import numpy as np
import ml_dtypes


def mxq(x, axis, fmt="e4m3"):
    dtype, down = {"e4m3": (ml_dtypes.float8_e4m3fn, 7), "e5m2": (ml_dtypes.float8_e5m2, 14)}[fmt]
    v = np.moveaxis(np.asarray(x, np.float32).astype(ml_dtypes.bfloat16).astype(np.float64), axis, -1)
    blocks = v.reshape(v.shape[:-1] + (-1, 32))
    amax = np.abs(blocks).max(-1, keepdims=True)
    byte = np.maximum(np.where(amax > 0, np.frexp(amax)[1] - 1 + 127, 0) - down, 1)
    scale = np.exp2(byte - 127.0)
    codes = (blocks / scale).astype(np.float32).astype(dtype).astype(np.float64)
    return np.moveaxis((codes * scale).reshape(v.shape), -1, axis)


WIDE = False


def mx_kscale(k):
    if not WIDE:
        return np.ones(k)
    levels = np.array([10, -10, 5, -5, 0])
    a = np.random.permutation(np.resize(levels, k // 512 * 4)).reshape(k // 512, 4)
    idx = np.arange(k)
    return np.exp2(a[idx // 512, idx % 128 // 32])


BF16 = ml_dtypes.bfloat16


def bf(x):
    return np.asarray(x, np.float32).astype(BF16)


def f64(x):
    return np.asarray(x).astype(np.float64)


B, N, D1, D2, NS = 64, 16, 1024, 256, 2
ND = D1
NP = N // NS


def rolled_concat(arrays, n, axis=-1):
    return np.concatenate(arrays[n:] + arrays[:n], axis=axis)


def setup_inputs():
    t = mx_kscale(NS * D2)
    tb = t.reshape(NS, D2)
    fac = np.stack([np.roll(tb, i, axis=0) for i in range(NS)])
    x2 = np.random.standard_normal((B, NS, NP, NS, NP, D2)) * fac[None, :, None, :, None, :]
    return {"in_1e": bf(np.random.standard_normal((B, N, D1))),
            "in_2e": bf(x2.reshape(B, N, N, D2)),
            "W_unmixed": bf(np.random.standard_normal((D1, ND)) * 0.6 / np.sqrt(D1)),
            "b_unmixed": bf(np.random.standard_normal(ND) * 0.3),
            "W_mixed": bf(np.random.standard_normal((NS * D1, ND)) * 0.6 * np.sqrt(NP) / np.sqrt(NS * D1)),
            "W_2e": bf(np.random.standard_normal((NS * D2, ND)) * 0.6 * np.sqrt(NP) / np.sqrt(NS * D2) / t[:, None])}


def reference(in_1e, in_2e, W_unmixed, b_unmixed, W_mixed, W_2e):
    x1, x2 = f64(in_1e), f64(in_2e)
    dense_unmixed = (mxq(x1, 2, "e4m3") @ mxq(f64(W_unmixed), 0, "e4m3")) + f64(b_unmixed)
    split_unmixed = np.split(dense_unmixed, NS, axis=-2)
    split_1e = np.split(x1, NS, axis=-2)
    split_means = [np.mean(s, axis=-2, keepdims=True) for s in split_1e]
    split_concat = [rolled_concat(split_means, i) for i in range(NS)]
    all_spins = np.concatenate(split_concat, axis=-2)
    dense_mixed = mxq(all_spins, 2, "e4m3") @ mxq(f64(W_mixed), 0, "e4m3")
    dense_mixed_split = np.split(dense_mixed, NS, axis=-2)
    split_2e = np.split(x2, NS, axis=-3)
    concat_2e = []
    for spin in range(NS):
        blocks = np.split(split_2e[spin], NS, axis=-2)
        means = [np.mean(p, axis=-2) for p in blocks]
        concat_2e.append(rolled_concat(means, spin))
    all_2e = np.concatenate(concat_2e, axis=-2)
    dense_2e = mxq(all_2e, 2, "e4m3") @ mxq(f64(W_2e), 0, "e4m3")
    dense_2e_split = np.split(dense_2e, NS, axis=-2)
    out_splits = [u + m + e for u, m, e in zip(split_unmixed, dense_mixed_split, dense_2e_split)]
    dense_out = np.concatenate(out_splits, axis=-2)
    return np.tanh(dense_out) + x1

@@ -1,0 +1,334 @@
+from contextlib import ExitStack
+
+import concourse.mybir as mybir
+from concourse.masks import make_identity
+
+F32 = mybir.dt.float32
+BF16 = mybir.dt.bfloat16
+U32 = mybir.dt.uint32
+U8 = mybir.dt.uint8
+FP8X4 = mybir.dt.float8_e4m3fn_x4
+ADD = mybir.AluOpType.add
+TANH = mybir.ActivationFunctionType.Tanh
+
+P = 128
+PACK = 4
+WALKERS = 64
+ELECTRONS = 16
+PER_SPIN = 8
+D1 = 1024
+D2 = 256
+TOKENS = WALKERS * ELECTRONS
+UNIT = 256
+UNITS = TOKENS // UNIT
+TILES_PER_UNIT = UNIT // P
+D_TILES = D1 // P
+BANK = 512
+HALF = D1 // 2
+WALKERS_PER_TILE = P // ELECTRONS
+
+WM = 0
+WU = 4
+W2 = 6
+SLABS = 7
+PAIR_TILES = TOKENS // P
+BIG_LOADS = SLABS + PAIR_TILES
+BIG_BUFS = 10
+
+FLOPS = 2 * (TOKENS * D1 * D1 + 2 * WALKERS * 2 * D1 * D1 + TOKENS * 2 * D2 * D1)
+
+
+def tile_ferminetoneelectronlayer_pa_kernel(
+    tc, in_1e, in_2e, W_unmixed, b_unmixed, W_mixed, W_2e, out
+):
+    nc = tc.nc
+    with ExitStack() as ctx:
+        const = ctx.enter_context(tc.tile_pool(name="const", bufs=1))
+        keep = ctx.enter_context(tc.tile_pool(name="keep", bufs=1))
+        big = ctx.enter_context(tc.tile_pool(name="big", bufs=BIG_BUFS))
+        stage = ctx.enter_context(tc.tile_pool(name="stage", bufs=2))
+        sums = ctx.enter_context(tc.tile_pool(name="sums", bufs=3))
+        acts = ctx.enter_context(tc.tile_pool(name="acts", bufs=8))
+        results = ctx.enter_context(tc.tile_pool(name="results", bufs=4))
+        in_ps = ctx.enter_context(tc.psum_pool(name="in_ps", bufs=2))
+        mm_ps = ctx.enter_context(tc.psum_pool(name="mm_ps", bufs=4))
+        out_ps = ctx.enter_context(tc.psum_pool(name="out_ps", bufs=2))
+
+        x1_rows = in_1e.rearrange("b i k -> (b i) k").rearrange("(t p) k -> p t k", p=P)
+        out_rows = out.rearrange("b i d -> (b i) d")
+        pair_rows = in_2e.rearrange("b i (jj j0) c -> (i jj) b (j0 c)", j0=2)
+        wm_slabs = W_mixed.rearrange("(g t p) n -> g p t n", t=PACK, p=P)
+        wu_slabs = W_unmixed.rearrange("(g u q e) n -> g q u e n", u=2, q=P, e=2)
+        w2_slab = W_2e.rearrange("(t p) n -> p t n", p=P)
+
+        bias_rows = const.tile([P, P], BF16)
+        nc.vector.memset(bias_rows[:], 0.0)
+        nc.scalar.dma_start(out=bias_rows[0:D_TILES, :], in_=b_unmixed.rearrange("(r c) -> r c", c=P))
+        x1 = keep.tile([P, TOKENS // P, D1], BF16)
+        for unit in range(UNITS):
+            tiles = slice(unit * TILES_PER_UNIT, (unit + 1) * TILES_PER_UNIT)
+            nc.sync.dma_start(out=x1[:, tiles, :], in_=x1_rows[:, tiles, :])
+
+        big_tiles = {}
+
+        def load_big(j):
+            if j < SLABS:
+                raw = big.tile([P, PACK, D1], BF16, tag="big", name="raw")
+                if j < WU:
+                    nc.sync.dma_start(out=raw[:], in_=wm_slabs[j - WM])
+                elif j < W2:
+                    for u in range(2):
+                        nc.sync.dma_start(
+                            out=raw[:, 2 * u : 2 * u + 2, :], in_=wu_slabs[j - WU][:, u, :, :]
+                        )
+                else:
+                    nc.sync.dma_start(out=raw[:], in_=w2_slab)
+            else:
+                first = (j - SLABS) * WALKERS_PER_TILE
+                raw = big.tile([P, WALKERS_PER_TILE, 2 * D2], BF16, tag="big", name="raw")
+                nc.sync.dma_start(out=raw[:], in_=pair_rows[:, first : first + WALKERS_PER_TILE, :])
+            big_tiles[j] = raw
+
+        for j in range(BIG_BUFS):
+            load_big(j)
+
+        ident = const.tile([P, P], F32)
+        make_identity(nc, ident[:])
+        ident_bf = const.tile([P, P], BF16)
+        nc.vector.tensor_copy(out=ident_bf[:], in_=ident[:])
+
+        hit_m = const.tile([P, 2 * WALKERS_PER_TILE], F32)
+        nc.vector.tensor_reduce(
+            out=hit_m[:],
+            in_=ident[:].rearrange("p (q i) -> p q i", i=PER_SPIN),
+            axis=mybir.AxisListType.X,
+            op=ADD,
+        )
+        sel_m = const.tile([P, 2, WALKERS_PER_TILE], BF16)
+        nc.vector.tensor_scalar_mul(
+            out=sel_m[:], in0=hit_m[:].rearrange("p (b s) -> p s b", s=2), scalar1=1.0 / PER_SPIN
+        )
+
+        hit_2 = const.tile([P, 2 * ELECTRONS], F32)
+        nc.vector.tensor_reduce(
+            out=hit_2[:],
+            in_=ident[:].rearrange("p (q j) -> p q j", j=PER_SPIN // 2),
+            axis=mybir.AxisListType.X,
+            op=ADD,
+        )
+        hit_2_by_spin = hit_2[:].rearrange("p (r i c) -> p r c i", r=2, c=2)
+        sel_2 = const.tile([P, 2, ELECTRONS], BF16)
+        for row_spin in range(2):
+            for place in range(2):
+                nc.vector.tensor_scalar_mul(
+                    out=sel_2[:, place, row_spin * PER_SPIN : (row_spin + 1) * PER_SPIN],
+                    in0=hit_2_by_spin[:, row_spin, (row_spin + place) % 2, :],
+                    scalar1=1.0 / PER_SPIN,
+                )
+
+        x_codes = keep.tile([P, UNITS, 2, UNIT], U32, align_bytes=64)
+        x_scales = keep.tile([P, UNITS, 2, UNIT], U8, align_bytes=64)
+        m_ps = []
+        for g in range(2):
+            m_bank = mm_ps.tile([P, PACK, P], F32, tag="mm_bank", name="m_bank")
+            m_ps.append(m_bank)
+        for unit in range(UNITS):
+            x_grouped = stage.tile([P, 2, UNIT, PACK], BF16, align_bytes=64)
+            for half in range(TILES_PER_UNIT):
+                tt = unit * TILES_PER_UNIT + half
+                tokens = slice(half * P, (half + 1) * P)
+                words = x1[:, tt, :].bitcast(F32)
+                xt = in_ps.tile([P, PACK, P], F32, tag="in_bank")
+                for c in range(PACK):
+                    nc.tensor.transpose(xt[:, c, :], words[:, c * P : (c + 1) * P], ident[:])
+                nc.scalar.copy(
+                    out=x_grouped[:].bitcast(F32)[:, :, tokens, :],
+                    in_=xt[:].rearrange("p (g u) r -> p g r u", u=2),
+                )
+                for c in range(D1 // P):
+                    nc.tensor.matmul(
+                        out=m_ps[c // PACK][:, c % PACK, :].rearrange("p (s b) -> p s b", s=2)[
+                            :, :, tt * WALKERS_PER_TILE : (tt + 1) * WALKERS_PER_TILE
+                        ],
+                        lhsT=x1[:, tt, c * P : (c + 1) * P],
+                        rhs=sel_m[:],
+                        start=True,
+                        stop=True,
+                    )
+            nc.vector.quantize_mx(
+                out=x_codes[:, unit, :, :].rearrange("p g r -> p (g r)").bitcast(FP8X4),
+                scales=x_scales[:, unit, :, :].rearrange("p g r -> p (g r)"),
+                in_=x_grouped[:].rearrange("p g r t -> p (g r t)"),
+            )
+
+        m_grouped = keep.tile([P, 2, 2 * P, PACK], BF16, align_bytes=64)
+        m_codes = keep.tile([P, 2, 2 * P], U32, align_bytes=64)
+        m_scales = keep.tile([P, 2, 2 * P], U8, align_bytes=64)
+        for g in range(2):
+            for rep in range(2):
+                nc.scalar.copy(
+                    out=m_grouped[:, g, rep * P : (rep + 1) * P, :],
+                    in_=m_ps[g][:].rearrange("p t c -> p c t"),
+                )
+        nc.vector.quantize_mx(
+            out=m_codes[:].rearrange("p g c -> p (g c)").bitcast(FP8X4),
+            scales=m_scales[:].rearrange("p g c -> p (g c)"),
+            in_=m_grouped[:].rearrange("p g c t -> p (g c t)"),
+        )
+
+        bias_ps = in_ps.tile([P, P], BF16, tag="in_bank")
+        nc.tensor.transpose(bias_ps[:], bias_rows[:], ident_bf[:])
+        bias = const.tile([P, D_TILES], F32)
+        nc.vector.tensor_copy(out=bias[:], in_=bias_ps[:, 0:D_TILES])
+
+        w_codes = keep.tile([P, SLABS, D1], U32, align_bytes=64)
+        w_scales = keep.tile([P, SLABS, D1], U8, align_bytes=64)
+        w_grouped = {}
+        for k in range(SLABS + 1):
+            if k < SLABS:
+                raw = big_tiles[k]
+                grouped = stage.tile([P, D1, PACK], BF16, align_bytes=64)
+                w_grouped[k] = grouped
+                nc.vector.tensor_copy(
+                    out=grouped[:, 0:HALF, :].rearrange("p (c i) t -> p c t i", i=4),
+                    in_=raw[:, :, 0:HALF].rearrange("p t (c i) -> p c t i", i=4),
+                )
+                nc.scalar.copy(
+                    out=grouped[:, HALF:D1, :].rearrange("p (c i) t -> p c t i", i=4),
+                    in_=raw[:, :, HALF:D1].rearrange("p t (c i) -> p c t i", i=4),
+                )
+                if k + BIG_BUFS < BIG_LOADS:
+                    load_big(k + BIG_BUFS)
+            if k > 0:
+                nc.vector.quantize_mx(
+                    out=w_codes[:, k - 1, :].bitcast(FP8X4),
+                    scales=w_scales[:, k - 1, :],
+                    in_=w_grouped[k - 1][:].rearrange("p n t -> p (n t)"),
+                )
+
+        g_bias = keep.tile([P, D_TILES, P], F32)
+        for bank in range(2):
+            g_bank = mm_ps.tile([P, PACK, P], F32, tag="mm_bank")
+            for j in range(PACK):
+                dt = bank * PACK + j
+                features = slice(dt * P, (dt + 1) * P)
+                for k in range(4):
+                    first = 0 if k < 2 else WALKERS
+                    nc.tensor.matmul_mx(
+                        out=g_bank[:, j, :],
+                        lhsT=w_codes[:, WM + k, features].bitcast(FP8X4),
+                        lhsT_scale=w_scales[:, WM + k, features],
+                        rhs=m_codes[:, k % 2, first : first + P].bitcast(FP8X4),
+                        rhs_scale=m_scales[:, k % 2, first : first + P],
+                        start=(k == 0),
+                        stop=(k == 3),
+                    )
+            dts = slice(bank * PACK, (bank + 1) * PACK)
+            nc.vector.tensor_tensor(
+                out=g_bias[:, dts, :].rearrange("p j (b s) -> p j b s", s=2),
+                in0=g_bank[:].rearrange("p j (s b) -> p j b s", s=2),
+                in1=bias[:, dts].unsqueeze(2).unsqueeze(3).to_broadcast([P, PACK, WALKERS, 2]),
+                op=ADD,
+            )
+
+        e_codes = keep.tile([P, UNITS, UNIT], U32, align_bytes=64)
+        e_scales = keep.tile([P, UNITS, UNIT], U8, align_bytes=64)
+
+        def pair_means(unit):
+            e_grouped = stage.tile([P, UNIT, PACK], BF16, align_bytes=64)
+            for half in range(TILES_PER_UNIT):
+                raw = big_tiles[SLABS + unit * TILES_PER_UNIT + half]
+                blocks = raw[:].rearrange("p w (j0 h c) -> p w j0 h c", j0=2, h=2)
+                e_bank = in_ps.tile([P, PACK, P], F32, tag="in_bank")
+                by_half = e_bank[:].rearrange("p (place h) r -> p h place r", h=2)
+                for w in range(WALKERS_PER_TILE):
+                    for h in range(2):
+                        for j0 in range(2):
+                            nc.tensor.matmul(
+                                out=by_half[:, h, :, w * ELECTRONS : (w + 1) * ELECTRONS],
+                                lhsT=blocks[:, w, j0, h, :],
+                                rhs=sel_2[:],
+                                start=(j0 == 0),
+                                stop=(j0 == 1),
+                            )
+                nc.scalar.copy(
+                    out=e_grouped[:, half * P : (half + 1) * P, :],
+                    in_=e_bank[:].rearrange("p t r -> p r t"),
+                )
+            nc.vector.quantize_mx(
+                out=e_codes[:, unit, :].bitcast(FP8X4),
+                scales=e_scales[:, unit, :],
+                in_=e_grouped[:].rearrange("p r t -> p (r t)"),
+            )
+
+        def layer(unit):
+            tanh_tiles = []
+            for pair in range(D_TILES // 2):
+                mm = mm_ps.tile([P, 2, UNIT], F32, tag="mm_bank")
+                for j in range(2):
+                    dt = 2 * pair + j
+                    features = slice(dt * P, (dt + 1) * P)
+                    for g in range(2):
+                        nc.tensor.matmul_mx(
+                            out=mm[:, j, :],
+                            lhsT=w_codes[:, WU + g, features].bitcast(FP8X4),
+                            lhsT_scale=w_scales[:, WU + g, features],
+                            rhs=x_codes[:, unit, g, :].bitcast(FP8X4),
+                            rhs_scale=x_scales[:, unit, g, :],
+                            start=(g == 0),
+                            stop=False,
+                        )
+                    nc.tensor.matmul_mx(
+                        out=mm[:, j, :],
+                        lhsT=w_codes[:, W2, features].bitcast(FP8X4),
+                        lhsT_scale=w_scales[:, W2, features],
+                        rhs=e_codes[:, unit, :].bitcast(FP8X4),
+                        rhs_scale=e_scales[:, unit, :],
+                        start=False,
+                        stop=True,
+                    )
+                groups = UNIT // PER_SPIN
+                total = sums.tile([P, 2, UNIT], F32)
+                nc.vector.tensor_tensor(
+                    out=total[:].rearrange("p j (c i) -> p j c i", i=PER_SPIN),
+                    in0=mm[:].rearrange("p j (c i) -> p j c i", i=PER_SPIN),
+                    in1=g_bias[:, 2 * pair : 2 * pair + 2, unit * groups : (unit + 1) * groups]
+                    .unsqueeze(3)
+                    .to_broadcast([P, 2, groups, PER_SPIN]),
+                    op=ADD,
+                )
+                tanh = acts.tile([P, 2, UNIT], F32)
+                nc.scalar.activation(out=tanh[:], in_=total[:], func=TANH)
+                tanh_tiles.append(tanh)
+            return tanh_tiles
+
+        def finish(unit, tanh_tiles):
+            rows = []
+            for half in range(TILES_PER_UNIT):
+                result = results.tile([P, D1], F32)
+                rows.append(result)
+            for bank in range(D1 // BANK):
+                for half in range(TILES_PER_UNIT):
+                    tt = unit * TILES_PER_UNIT + half
+                    back = out_ps.tile([P, PACK, P], F32)
+                    for j in range(PACK):
+                        dt = bank * PACK + j
+                        nc.tensor.transpose(
+                            back[:, j, :],
+                            tanh_tiles[dt // 2][:, dt % 2, half * P : (half + 1) * P],
+                            ident[:],
+                        )
+                    cols = slice(bank * BANK, (bank + 1) * BANK)
+                    nc.vector.tensor_tensor(
+                        out=rows[half][:, cols],
+                        in0=back[:].rearrange("p j c -> p (j c)"),
+                        in1=x1[:, tt, cols],
+                        op=ADD,
+                    )
+            for half in range(TILES_PER_UNIT):
+                tt = unit * TILES_PER_UNIT + half
+                nc.sync.dma_start(out=out_rows[tt * P : (tt + 1) * P, :], in_=rows[half][:])
+
+        for unit in range(UNITS):
+            pair_means(unit)
+            finish(unit, layer(unit))

@@ -53,6 +53,7 @@ def tile_ferminetoneelectronlayer_pa_kernel(
         in_ps = ctx.enter_context(tc.psum_pool(name="in_ps", bufs=2))
         mm_ps = ctx.enter_context(tc.psum_pool(name="mm_ps", bufs=4))
         out_ps = ctx.enter_context(tc.psum_pool(name="out_ps", bufs=2))
+        ctx.enter_context(tc.manual_schedule())
 
         x1_rows = in_1e.rearrange("b i k -> (b i) k").rearrange("(t p) k -> p t k", p=P)
         out_rows = out.rearrange("b i d -> (b i) d")
@@ -65,9 +66,6 @@ def tile_ferminetoneelectronlayer_pa_kernel(
         nc.vector.memset(bias_rows[:], 0.0)
         nc.scalar.dma_start(out=bias_rows[0:D_TILES, :], in_=b_unmixed.rearrange("(r c) -> r c", c=P))
         x1 = keep.tile([P, TOKENS // P, D1], BF16)
-        for unit in range(UNITS):
-            tiles = slice(unit * TILES_PER_UNIT, (unit + 1) * TILES_PER_UNIT)
-            nc.sync.dma_start(out=x1[:, tiles, :], in_=x1_rows[:, tiles, :])
 
         big_tiles = {}
 
@@ -89,7 +87,11 @@ def tile_ferminetoneelectronlayer_pa_kernel(
                 nc.sync.dma_start(out=raw[:], in_=pair_rows[:, first : first + WALKERS_PER_TILE, :])
             big_tiles[j] = raw
 
-        for j in range(BIG_BUFS):
+        load_big(0)
+        for unit in range(UNITS):
+            tiles = slice(unit * TILES_PER_UNIT, (unit + 1) * TILES_PER_UNIT)
+            nc.sync.dma_start(out=x1[:, tiles, :], in_=x1_rows[:, tiles, :])
+        for j in range(1, BIG_BUFS):
             load_big(j)
 
         ident = const.tile([P, P], F32)
@@ -126,14 +128,39 @@ def tile_ferminetoneelectronlayer_pa_kernel(
                     scalar1=1.0 / PER_SPIN,
                 )
 
+        w_codes = keep.tile([P, SLABS, D1], U32, align_bytes=64)
+        w_scales = keep.tile([P, SLABS, D1], U8, align_bytes=64)
+        w_grouped = {}
+
+        def regroup(k):
+            raw = big_tiles[k]
+            grouped = stage.tile([P, D1, PACK], BF16, align_bytes=64)
+            w_grouped[k] = grouped
+            nc.vector.tensor_copy(
+                out=grouped[:, 0:HALF, :].rearrange("p (c i) t -> p c t i", i=4),
+                in_=raw[:, :, 0:HALF].rearrange("p t (c i) -> p c t i", i=4),
+            )
+            nc.scalar.copy(
+                out=grouped[:, HALF:D1, :].rearrange("p (c i) t -> p c t i", i=4),
+                in_=raw[:, :, HALF:D1].rearrange("p t (c i) -> p c t i", i=4),
+            )
+            if k + BIG_BUFS < BIG_LOADS:
+                load_big(k + BIG_BUFS)
+
+        def quantise(k):
+            nc.vector.quantize_mx(
+                out=w_codes[:, k, :].bitcast(FP8X4),
+                scales=w_scales[:, k, :],
+                in_=w_grouped[k][:].rearrange("p n t -> p (n t)"),
+            )
+
         x_codes = keep.tile([P, UNITS, 2, UNIT], U32, align_bytes=64)
         x_scales = keep.tile([P, UNITS, 2, UNIT], U8, align_bytes=64)
-        m_ps = []
-        for g in range(2):
-            m_bank = mm_ps.tile([P, PACK, P], F32, tag="mm_bank", name="m_bank")
-            m_ps.append(m_bank)
-        for unit in range(UNITS):
-            x_grouped = stage.tile([P, 2, UNIT, PACK], BF16, align_bytes=64)
+        x_grouped = {}
+
+        def turn_x(unit):
+            grouped_x = stage.tile([P, 2, UNIT, PACK], BF16, align_bytes=64)
+            x_grouped[unit] = grouped_x
             for half in range(TILES_PER_UNIT):
                 tt = unit * TILES_PER_UNIT + half
                 tokens = slice(half * P, (half + 1) * P)
@@ -142,73 +169,76 @@ def tile_ferminetoneelectronlayer_pa_kernel(
                 for c in range(PACK):
                     nc.tensor.transpose(xt[:, c, :], words[:, c * P : (c + 1) * P], ident[:])
                 nc.scalar.copy(
-                    out=x_grouped[:].bitcast(F32)[:, :, tokens, :],
+                    out=grouped_x[:].bitcast(F32)[:, :, tokens, :],
                     in_=xt[:].rearrange("p (g u) r -> p g r u", u=2),
                 )
-                for c in range(D1 // P):
-                    nc.tensor.matmul(
-                        out=m_ps[c // PACK][:, c % PACK, :].rearrange("p (s b) -> p s b", s=2)[
-                            :, :, tt * WALKERS_PER_TILE : (tt + 1) * WALKERS_PER_TILE
-                        ],
-                        lhsT=x1[:, tt, c * P : (c + 1) * P],
-                        rhs=sel_m[:],
-                        start=True,
-                        stop=True,
-                    )
+
+        def quantise_x(unit):
             nc.vector.quantize_mx(
                 out=x_codes[:, unit, :, :].rearrange("p g r -> p (g r)").bitcast(FP8X4),
                 scales=x_scales[:, unit, :, :].rearrange("p g r -> p (g r)"),
-                in_=x_grouped[:].rearrange("p g r t -> p (g r t)"),
+                in_=x_grouped[unit][:].rearrange("p g r t -> p (g r t)"),
             )
 
+        regroup(0)
+        turn_x(0)
+        quantise(0)
+        turn_x(1)
+        quantise_x(0)
+        turn_x(2)
+        quantise_x(1)
+        regroup(1)
+        turn_x(3)
+        quantise_x(2)
+        quantise(1)
+        quantise_x(3)
+
+        m_ps = []
+        for g in range(2):
+            m_bank = mm_ps.tile([P, PACK, P], F32, tag="mm_bank", name="m_bank")
+            m_ps.append(m_bank)
+        for tt in range(TOKENS // P):
+            for c in range(D1 // P):
+                nc.tensor.matmul(
+                    out=m_ps[c // PACK][:, c % PACK, :].rearrange("p (s b) -> p s b", s=2)[
+                        :, :, tt * WALKERS_PER_TILE : (tt + 1) * WALKERS_PER_TILE
+                    ],
+                    lhsT=x1[:, tt, c * P : (c + 1) * P],
+                    rhs=sel_m[:],
+                    start=True,
+                    stop=True,
+                )
+        regroup(2)
         m_grouped = keep.tile([P, 2, 2 * P, PACK], BF16, align_bytes=64)
         m_codes = keep.tile([P, 2, 2 * P], U32, align_bytes=64)
         m_scales = keep.tile([P, 2, 2 * P], U8, align_bytes=64)
         for g in range(2):
-            for rep in range(2):
-                nc.scalar.copy(
-                    out=m_grouped[:, g, rep * P : (rep + 1) * P, :],
-                    in_=m_ps[g][:].rearrange("p t c -> p c t"),
-                )
+            nc.scalar.copy(
+                out=m_grouped[:, g, 0:P, :],
+                in_=m_ps[g][:].rearrange("p t c -> p c t"),
+            )
+        quantise(2)
+        nc.vector.tensor_copy(out=m_grouped[:, :, P : 2 * P, :], in_=m_grouped[:, :, 0:P, :])
+        regroup(3)
         nc.vector.quantize_mx(
             out=m_codes[:].rearrange("p g c -> p (g c)").bitcast(FP8X4),
             scales=m_scales[:].rearrange("p g c -> p (g c)"),
             in_=m_grouped[:].rearrange("p g c t -> p (g c t)"),
         )
+        quantise(3)
 
         bias_ps = in_ps.tile([P, P], BF16, tag="in_bank")
         nc.tensor.transpose(bias_ps[:], bias_rows[:], ident_bf[:])
         bias = const.tile([P, D_TILES], F32)
         nc.vector.tensor_copy(out=bias[:], in_=bias_ps[:, 0:D_TILES])
 
-        w_codes = keep.tile([P, SLABS, D1], U32, align_bytes=64)
-        w_scales = keep.tile([P, SLABS, D1], U8, align_bytes=64)
-        w_grouped = {}
-        for k in range(SLABS + 1):
-            if k < SLABS:
-                raw = big_tiles[k]
-                grouped = stage.tile([P, D1, PACK], BF16, align_bytes=64)
-                w_grouped[k] = grouped
-                nc.vector.tensor_copy(
-                    out=grouped[:, 0:HALF, :].rearrange("p (c i) t -> p c t i", i=4),
-                    in_=raw[:, :, 0:HALF].rearrange("p t (c i) -> p c t i", i=4),
-                )
-                nc.scalar.copy(
-                    out=grouped[:, HALF:D1, :].rearrange("p (c i) t -> p c t i", i=4),
-                    in_=raw[:, :, HALF:D1].rearrange("p t (c i) -> p c t i", i=4),
-                )
-                if k + BIG_BUFS < BIG_LOADS:
-                    load_big(k + BIG_BUFS)
-            if k > 0:
-                nc.vector.quantize_mx(
-                    out=w_codes[:, k - 1, :].bitcast(FP8X4),
-                    scales=w_scales[:, k - 1, :],
-                    in_=w_grouped[k - 1][:].rearrange("p n t -> p (n t)"),
-                )
+        regroup(WU)
 
         g_bias = keep.tile([P, D_TILES, P], F32)
+        g_banks = []
         for bank in range(2):
-            g_bank = mm_ps.tile([P, PACK, P], F32, tag="mm_bank")
+            g_bank = mm_ps.tile([P, PACK, P], F32, tag="mm_bank", name="g_bank")
+            g_banks.append(g_bank)
             for j in range(PACK):
                 dt = bank * PACK + j
                 features = slice(dt * P, (dt + 1) * P)
@@ -223,112 +253,138 @@ def tile_ferminetoneelectronlayer_pa_kernel(
                         start=(k == 0),
                         stop=(k == 3),
                     )
+        regroup(WU + 1)
+        quantise(WU)
+        for bank in range(2):
             dts = slice(bank * PACK, (bank + 1) * PACK)
             nc.vector.tensor_tensor(
                 out=g_bias[:, dts, :].rearrange("p j (b s) -> p j b s", s=2),
-                in0=g_bank[:].rearrange("p j (s b) -> p j b s", s=2),
+                in0=g_banks[bank][:].rearrange("p j (s b) -> p j b s", s=2),
                 in1=bias[:, dts].unsqueeze(2).unsqueeze(3).to_broadcast([P, PACK, WALKERS, 2]),
                 op=ADD,
             )
 
+        regroup(W2)
+        quantise(WU + 1)
+        quantise(W2)
+
         e_codes = keep.tile([P, UNITS, UNIT], U32, align_bytes=64)
         e_scales = keep.tile([P, UNITS, UNIT], U8, align_bytes=64)
 
-        def pair_means(unit):
-            e_grouped = stage.tile([P, UNIT, PACK], BF16, align_bytes=64)
-            for half in range(TILES_PER_UNIT):
-                raw = big_tiles[SLABS + unit * TILES_PER_UNIT + half]
-                blocks = raw[:].rearrange("p w (j0 h c) -> p w j0 h c", j0=2, h=2)
-                e_bank = in_ps.tile([P, PACK, P], F32, tag="in_bank")
-                by_half = e_bank[:].rearrange("p (place h) r -> p h place r", h=2)
-                for w in range(WALKERS_PER_TILE):
-                    for h in range(2):
-                        for j0 in range(2):
-                            nc.tensor.matmul(
-                                out=by_half[:, h, :, w * ELECTRONS : (w + 1) * ELECTRONS],
-                                lhsT=blocks[:, w, j0, h, :],
-                                rhs=sel_2[:],
-                                start=(j0 == 0),
-                                stop=(j0 == 1),
-                            )
-                nc.scalar.copy(
-                    out=e_grouped[:, half * P : (half + 1) * P, :],
-                    in_=e_bank[:].rearrange("p t r -> p r t"),
-                )
-            nc.vector.quantize_mx(
-                out=e_codes[:, unit, :].bitcast(FP8X4),
-                scales=e_scales[:, unit, :],
-                in_=e_grouped[:].rearrange("p r t -> p (r t)"),
-            )
+        e_grouped = {}
+        e_banks = {}
 
-        def layer(unit):
-            tanh_tiles = []
-            for pair in range(D_TILES // 2):
-                mm = mm_ps.tile([P, 2, UNIT], F32, tag="mm_bank")
-                for j in range(2):
-                    dt = 2 * pair + j
-                    features = slice(dt * P, (dt + 1) * P)
-                    for g in range(2):
-                        nc.tensor.matmul_mx(
-                            out=mm[:, j, :],
-                            lhsT=w_codes[:, WU + g, features].bitcast(FP8X4),
-                            lhsT_scale=w_scales[:, WU + g, features],
-                            rhs=x_codes[:, unit, g, :].bitcast(FP8X4),
-                            rhs_scale=x_scales[:, unit, g, :],
-                            start=(g == 0),
-                            stop=False,
+        def pair_means(quarter):
+            unit = quarter // 4
+            half = quarter % 4 // 2
+            tile_index = quarter // 2
+            if quarter % 4 == 0:
+                grouped_e = stage.tile([P, UNIT, PACK], BF16, align_bytes=64)
+                e_grouped[unit] = grouped_e
+            if quarter % 2 == 0:
+                e_bank = in_ps.tile([P, PACK, P], F32, tag="in_bank")
+                e_banks[tile_index] = e_bank
+            blocks = big_tiles[SLABS + tile_index][:].rearrange("p w (j0 h c) -> p w j0 h c", j0=2, h=2)
+            by_half = e_banks[tile_index][:].rearrange("p (place h) r -> p h place r", h=2)
+            for w in range(quarter % 2 * 4, quarter % 2 * 4 + 4):
+                for h in range(2):
+                    for j0 in range(2):
+                        nc.tensor.matmul(
+                            out=by_half[:, h, :, w * ELECTRONS : (w + 1) * ELECTRONS],
+                            lhsT=blocks[:, w, j0, h, :],
+                            rhs=sel_2[:],
+                            start=(j0 == 0),
+                            stop=(j0 == 1),
                         )
+            if quarter % 2 == 1:
+                nc.scalar.copy(
+                    out=e_grouped[unit][:, half * P : (half + 1) * P, :],
+                    in_=e_banks[tile_index][:].rearrange("p t r -> p r t"),
+                )
+            if quarter % 4 == 3:
+                nc.vector.quantize_mx(
+                    out=e_codes[:, unit, :].bitcast(FP8X4),
+                    scales=e_scales[:, unit, :],
+                    in_=e_grouped[unit][:].rearrange("p r t -> p (r t)"),
+                )
+
+        tanh_tiles = {}
+
+        def layer(step):
+            unit = step // 4
+            pair = step % 4
+            mm = mm_ps.tile([P, 2, UNIT], F32, tag="mm_bank")
+            for j in range(2):
+                dt = 2 * pair + j
+                features = slice(dt * P, (dt + 1) * P)
+                for g in range(2):
                     nc.tensor.matmul_mx(
                         out=mm[:, j, :],
-                        lhsT=w_codes[:, W2, features].bitcast(FP8X4),
-                        lhsT_scale=w_scales[:, W2, features],
-                        rhs=e_codes[:, unit, :].bitcast(FP8X4),
-                        rhs_scale=e_scales[:, unit, :],
-                        start=False,
-                        stop=True,
+                        lhsT=w_codes[:, WU + g, features].bitcast(FP8X4),
+                        lhsT_scale=w_scales[:, WU + g, features],
+                        rhs=x_codes[:, unit, g, :].bitcast(FP8X4),
+                        rhs_scale=x_scales[:, unit, g, :],
+                        start=(g == 0),
+                        stop=False,
                     )
-                groups = UNIT // PER_SPIN
-                total = sums.tile([P, 2, UNIT], F32)
-                nc.vector.tensor_tensor(
-                    out=total[:].rearrange("p j (c i) -> p j c i", i=PER_SPIN),
-                    in0=mm[:].rearrange("p j (c i) -> p j c i", i=PER_SPIN),
-                    in1=g_bias[:, 2 * pair : 2 * pair + 2, unit * groups : (unit + 1) * groups]
-                    .unsqueeze(3)
-                    .to_broadcast([P, 2, groups, PER_SPIN]),
-                    op=ADD,
+                nc.tensor.matmul_mx(
+                    out=mm[:, j, :],
+                    lhsT=w_codes[:, W2, features].bitcast(FP8X4),
+                    lhsT_scale=w_scales[:, W2, features],
+                    rhs=e_codes[:, unit, :].bitcast(FP8X4),
+                    rhs_scale=e_scales[:, unit, :],
+                    start=False,
+                    stop=True,
                 )
-                tanh = acts.tile([P, 2, UNIT], F32)
-                nc.scalar.activation(out=tanh[:], in_=total[:], func=TANH)
-                tanh_tiles.append(tanh)
-            return tanh_tiles
+            groups = UNIT // PER_SPIN
+            total = sums.tile([P, 2, UNIT], F32)
+            nc.vector.tensor_tensor(
+                out=total[:].rearrange("p j (c i) -> p j c i", i=PER_SPIN),
+                in0=mm[:].rearrange("p j (c i) -> p j c i", i=PER_SPIN),
+                in1=g_bias[:, 2 * pair : 2 * pair + 2, unit * groups : (unit + 1) * groups]
+                .unsqueeze(3)
+                .to_broadcast([P, 2, groups, PER_SPIN]),
+                op=ADD,
+            )
+            tanh = acts.tile([P, 2, UNIT], F32)
+            nc.scalar.activation(out=tanh[:], in_=total[:], func=TANH)
+            tanh_tiles[step] = tanh
 
-        def finish(unit, tanh_tiles):
-            rows = []
-            for half in range(TILES_PER_UNIT):
+        rows = {}
+
+        def finish(step):
+            unit = step // 4
+            bank = step % 4 // 2
+            half = step % 2
+            tt = unit * TILES_PER_UNIT + half
+            if bank == 0:
                 result = results.tile([P, D1], F32)
-                rows.append(result)
-            for bank in range(D1 // BANK):
-                for half in range(TILES_PER_UNIT):
-                    tt = unit * TILES_PER_UNIT + half
-                    back = out_ps.tile([P, PACK, P], F32)
-                    for j in range(PACK):
-                        dt = bank * PACK + j
-                        nc.tensor.transpose(
-                            back[:, j, :],
-                            tanh_tiles[dt // 2][:, dt % 2, half * P : (half + 1) * P],
-                            ident[:],
-                        )
-                    cols = slice(bank * BANK, (bank + 1) * BANK)
-                    nc.vector.tensor_tensor(
-                        out=rows[half][:, cols],
-                        in0=back[:].rearrange("p j c -> p (j c)"),
-                        in1=x1[:, tt, cols],
-                        op=ADD,
-                    )
-            for half in range(TILES_PER_UNIT):
-                tt = unit * TILES_PER_UNIT + half
-                nc.sync.dma_start(out=out_rows[tt * P : (tt + 1) * P, :], in_=rows[half][:])
+                rows[tt] = result
+            back = out_ps.tile([P, PACK, P], F32)
+            for j in range(PACK):
+                dt = bank * PACK + j
+                nc.tensor.transpose(
+                    back[:, j, :],
+                    tanh_tiles[4 * unit + dt // 2][:, dt % 2, half * P : (half + 1) * P],
+                    ident[:],
+                )
+            cols = slice(bank * BANK, (bank + 1) * BANK)
+            nc.vector.tensor_tensor(
+                out=rows[tt][:, cols],
+                in0=back[:].rearrange("p j c -> p (j c)"),
+                in1=x1[:, tt, cols],
+                op=ADD,
+            )
+            if bank == 1:
+                nc.sync.dma_start(out=out_rows[tt * P : (tt + 1) * P, :], in_=rows[tt][:])
 
-        for unit in range(UNITS):
-            pair_means(unit)
-            finish(unit, layer(unit))
+        steps = 4 * UNITS
+        for quarter in range(5):
+            pair_means(quarter)
+        for step in range(steps + 3):
+            if step < steps:
+                layer(step)
+            if step >= 3:
+                finish(step - 3)
+            if step + 5 < steps:
+                pair_means(step + 5)

@@ -24,8 +24,9 @@ UNITS = TOKENS // UNIT
 TILES_PER_UNIT = UNIT // P
 D_TILES = D1 // P
 BANK = 512
-HALF = D1 // 2
+V_COLS = (640, 640, 640, 384, 384, 384, 384)
 WALKERS_PER_TILE = P // ELECTRONS
+GROUPS = UNIT // PER_SPIN
 
 WM = 0
 WU = 4
@@ -33,7 +34,7 @@ W2 = 6
 SLABS = 7
 PAIR_TILES = TOKENS // P
 BIG_LOADS = SLABS + PAIR_TILES
-BIG_BUFS = 10
+BIG_BUFS = 9
 
 FLOPS = 2 * (TOKENS * D1 * D1 + 2 * WALKERS * 2 * D1 * D1 + TOKENS * 2 * D2 * D1)
 
@@ -47,16 +48,16 @@ def tile_ferminetoneelectronlayer_pa_kernel(
         keep = ctx.enter_context(tc.tile_pool(name="keep", bufs=1))
         big = ctx.enter_context(tc.tile_pool(name="big", bufs=BIG_BUFS))
         stage = ctx.enter_context(tc.tile_pool(name="stage", bufs=2))
-        sums = ctx.enter_context(tc.tile_pool(name="sums", bufs=3))
-        acts = ctx.enter_context(tc.tile_pool(name="acts", bufs=8))
-        results = ctx.enter_context(tc.tile_pool(name="results", bufs=4))
+        sums = ctx.enter_context(tc.tile_pool(name="sums", bufs=2))
+        acts = ctx.enter_context(tc.tile_pool(name="acts", bufs=2))
+        results = ctx.enter_context(tc.tile_pool(name="results", bufs=3))
         in_ps = ctx.enter_context(tc.psum_pool(name="in_ps", bufs=2))
         mm_ps = ctx.enter_context(tc.psum_pool(name="mm_ps", bufs=4))
-        out_ps = ctx.enter_context(tc.psum_pool(name="out_ps", bufs=2))
+        g_ps = ctx.enter_context(tc.psum_pool(name="g_ps", bufs=2))
         ctx.enter_context(tc.manual_schedule())
 
-        x1_rows = in_1e.rearrange("b i k -> (b i) k").rearrange("(t p) k -> p t k", p=P)
-        out_rows = out.rearrange("b i d -> (b i) d")
+        x1_rows = in_1e.rearrange("b i k -> (b i) k").rearrange("(u p e) k -> u p e k", p=P, e=2)
+        out_rows = out.rearrange("b i d -> (b i) d").rearrange("(u p e) d -> u p e d", p=P, e=2)
         pair_rows = in_2e.rearrange("b i (jj j0) c -> (i jj) b (j0 c)", j0=2)
         wm_slabs = W_mixed.rearrange("(g t p) n -> g p t n", t=PACK, p=P)
         wu_slabs = W_unmixed.rearrange("(g u q e) n -> g q u e n", u=2, q=P, e=2)
@@ -65,14 +66,17 @@ def tile_ferminetoneelectronlayer_pa_kernel(
         bias_rows = const.tile([P, P], BF16)
         nc.vector.memset(bias_rows[:], 0.0)
         nc.scalar.dma_start(out=bias_rows[0:D_TILES, :], in_=b_unmixed.rearrange("(r c) -> r c", c=P))
-        x1 = keep.tile([P, TOKENS // P, D1], BF16)
+        x1 = keep.tile([P, UNITS, 2, D1], BF16)
 
         big_tiles = {}
 
         def load_big(j):
             if j < SLABS:
                 raw = big.tile([P, PACK, D1], BF16, tag="big", name="raw")
-                if j < WU:
+                if j == 0:
+                    for cols in (slice(0, V_COLS[0]), slice(V_COLS[0], D1)):
+                        nc.sync.dma_start(out=raw[:, :, cols], in_=wm_slabs[0][:, :, cols])
+                elif j < WU:
                     nc.sync.dma_start(out=raw[:], in_=wm_slabs[j - WM])
                 elif j < W2:
                     for u in range(2):
@@ -88,25 +92,28 @@ def tile_ferminetoneelectronlayer_pa_kernel(
             big_tiles[j] = raw
 
         load_big(0)
+        load_big(1)
         for unit in range(UNITS):
-            tiles = slice(unit * TILES_PER_UNIT, (unit + 1) * TILES_PER_UNIT)
-            nc.sync.dma_start(out=x1[:, tiles, :], in_=x1_rows[:, tiles, :])
-        for j in range(1, BIG_BUFS):
+            nc.sync.dma_start(out=x1[:, unit, :, :], in_=x1_rows[unit])
+        for j in range(2, BIG_BUFS):
             load_big(j)
 
+        dummy = const.tile([P, 1], F32)
+        nc.vector.memset(dummy[:], 0.0)
+        nc.scalar.activation(out=dummy[:], in_=dummy[:], func=TANH)
         ident = const.tile([P, P], F32)
         make_identity(nc, ident[:])
         ident_bf = const.tile([P, P], BF16)
         nc.vector.tensor_copy(out=ident_bf[:], in_=ident[:])
 
-        hit_m = const.tile([P, 2 * WALKERS_PER_TILE], F32)
+        hit_m = const.tile([P, GROUPS], F32)
         nc.vector.tensor_reduce(
             out=hit_m[:],
-            in_=ident[:].rearrange("p (q i) -> p q i", i=PER_SPIN),
+            in_=ident[:].rearrange("p (q i) -> p q i", i=PER_SPIN // 2),
             axis=mybir.AxisListType.X,
             op=ADD,
         )
-        sel_m = const.tile([P, 2, WALKERS_PER_TILE], BF16)
+        sel_m = const.tile([P, 2, GROUPS // 2], BF16)
         nc.vector.tensor_scalar_mul(
             out=sel_m[:], in0=hit_m[:].rearrange("p (b s) -> p s b", s=2), scalar1=1.0 / PER_SPIN
         )
@@ -134,15 +141,16 @@ def tile_ferminetoneelectronlayer_pa_kernel(
 
         def regroup(k):
             raw = big_tiles[k]
-            grouped = stage.tile([P, D1, PACK], BF16, align_bytes=64)
+            grouped = stage.tile([P, D1, PACK], BF16, align_bytes=64, bufs=3)
             w_grouped[k] = grouped
+            mid = V_COLS[k]
             nc.vector.tensor_copy(
-                out=grouped[:, 0:HALF, :].rearrange("p (c i) t -> p c t i", i=4),
-                in_=raw[:, :, 0:HALF].rearrange("p t (c i) -> p c t i", i=4),
+                out=grouped[:, 0:mid, :].rearrange("p (c i) t -> p c t i", i=4),
+                in_=raw[:, :, 0:mid].rearrange("p t (c i) -> p c t i", i=4),
             )
             nc.scalar.copy(
-                out=grouped[:, HALF:D1, :].rearrange("p (c i) t -> p c t i", i=4),
-                in_=raw[:, :, HALF:D1].rearrange("p t (c i) -> p c t i", i=4),
+                out=grouped[:, mid:D1, :].rearrange("p (c i) t -> p c t i", i=4),
+                in_=raw[:, :, mid:D1].rearrange("p t (c i) -> p c t i", i=4),
             )
             if k + BIG_BUFS < BIG_LOADS:
                 load_big(k + BIG_BUFS)
@@ -162,10 +170,10 @@ def tile_ferminetoneelectronlayer_pa_kernel(
             grouped_x = stage.tile([P, 2, UNIT, PACK], BF16, align_bytes=64)
             x_grouped[unit] = grouped_x
             for half in range(TILES_PER_UNIT):
-                tt = unit * TILES_PER_UNIT + half
                 tokens = slice(half * P, (half + 1) * P)
-                words = x1[:, tt, :].bitcast(F32)
-                xt = in_ps.tile([P, PACK, P], F32, tag="in_bank")
+                words = x1[:, unit, half, :].bitcast(F32)
+                ps, tag = ((in_ps, "in_bank"), (g_ps, "g_bank"))[half]
+                xt = ps.tile([P, PACK, P], F32, tag=tag, name="xt")
                 for c in range(PACK):
                     nc.tensor.transpose(xt[:, c, :], words[:, c * P : (c + 1) * P], ident[:])
                 nc.scalar.copy(
@@ -180,113 +188,125 @@ def tile_ferminetoneelectronlayer_pa_kernel(
                 in_=x_grouped[unit][:].rearrange("p g r t -> p (g r t)"),
             )
 
-        regroup(0)
-        turn_x(0)
-        quantise(0)
-        turn_x(1)
-        quantise_x(0)
-        turn_x(2)
-        quantise_x(1)
-        regroup(1)
-        turn_x(3)
-        quantise_x(2)
-        quantise(1)
-        quantise_x(3)
-
         m_ps = []
-        for g in range(2):
-            m_bank = mm_ps.tile([P, PACK, P], F32, tag="mm_bank", name="m_bank")
-            m_ps.append(m_bank)
-        for tt in range(TOKENS // P):
-            for c in range(D1 // P):
-                nc.tensor.matmul(
-                    out=m_ps[c // PACK][:, c % PACK, :].rearrange("p (s b) -> p s b", s=2)[
-                        :, :, tt * WALKERS_PER_TILE : (tt + 1) * WALKERS_PER_TILE
-                    ],
-                    lhsT=x1[:, tt, c * P : (c + 1) * P],
-                    rhs=sel_m[:],
-                    start=True,
-                    stop=True,
-                )
-        regroup(2)
         m_grouped = keep.tile([P, 2, 2 * P, PACK], BF16, align_bytes=64)
         m_codes = keep.tile([P, 2, 2 * P], U32, align_bytes=64)
         m_scales = keep.tile([P, 2, 2 * P], U8, align_bytes=64)
-        for g in range(2):
-            nc.scalar.copy(
-                out=m_grouped[:, g, 0:P, :],
-                in_=m_ps[g][:].rearrange("p t c -> p c t"),
+
+        def mean_m(unit):
+            if unit == 0:
+                for g in range(2):
+                    m_bank = mm_ps.tile([P, PACK, P], F32, tag="mm_bank", name="m_bank")
+                    m_ps.append(m_bank)
+            for c in range(D1 // P):
+                for half in range(2):
+                    nc.tensor.matmul(
+                        out=m_ps[c // PACK][:, c % PACK, :].rearrange("p (s b) -> p s b", s=2)[
+                            :, :, unit * GROUPS // 2 : (unit + 1) * GROUPS // 2
+                        ],
+                        lhsT=x1[:, unit, half, c * P : (c + 1) * P],
+                        rhs=sel_m[:],
+                        start=(half == 0),
+                        stop=(half == 1),
+                    )
+
+        def copy_m():
+            for g in range(2):
+                nc.scalar.copy(
+                    out=m_grouped[:, g, 0:P, :],
+                    in_=m_ps[g][:].rearrange("p t c -> p c t"),
+                )
+
+        def quantise_m():
+            nc.vector.tensor_copy(out=m_grouped[:, :, P : 2 * P, :], in_=m_grouped[:, :, 0:P, :])
+            nc.vector.quantize_mx(
+                out=m_codes[:].rearrange("p g c -> p (g c)").bitcast(FP8X4),
+                scales=m_scales[:].rearrange("p g c -> p (g c)"),
+                in_=m_grouped[:].rearrange("p g c t -> p (g c t)"),
             )
-        quantise(2)
-        nc.vector.tensor_copy(out=m_grouped[:, :, P : 2 * P, :], in_=m_grouped[:, :, 0:P, :])
-        regroup(3)
-        nc.vector.quantize_mx(
-            out=m_codes[:].rearrange("p g c -> p (g c)").bitcast(FP8X4),
-            scales=m_scales[:].rearrange("p g c -> p (g c)"),
-            in_=m_grouped[:].rearrange("p g c t -> p (g c t)"),
-        )
-        quantise(3)
 
-        bias_ps = in_ps.tile([P, P], BF16, tag="in_bank")
-        nc.tensor.transpose(bias_ps[:], bias_rows[:], ident_bf[:])
         bias = const.tile([P, D_TILES], F32)
-        nc.vector.tensor_copy(out=bias[:], in_=bias_ps[:, 0:D_TILES])
 
-        regroup(WU)
+        def turn_bias():
+            bias_ps = in_ps.tile([P, P], BF16, tag="in_bank")
+            nc.tensor.transpose(bias_ps[:], bias_rows[:], ident_bf[:])
+            nc.vector.tensor_copy(out=bias[:], in_=bias_ps[:, 0:D_TILES])
 
         g_bias = keep.tile([P, D_TILES, P], F32)
         g_banks = []
-        for bank in range(2):
-            g_bank = mm_ps.tile([P, PACK, P], F32, tag="mm_bank", name="g_bank")
-            g_banks.append(g_bank)
-            for j in range(PACK):
-                dt = bank * PACK + j
-                features = slice(dt * P, (dt + 1) * P)
-                for k in range(4):
-                    first = 0 if k < 2 else WALKERS
-                    nc.tensor.matmul_mx(
-                        out=g_bank[:, j, :],
-                        lhsT=w_codes[:, WM + k, features].bitcast(FP8X4),
-                        lhsT_scale=w_scales[:, WM + k, features],
-                        rhs=m_codes[:, k % 2, first : first + P].bitcast(FP8X4),
-                        rhs_scale=m_scales[:, k % 2, first : first + P],
-                        start=(k == 0),
-                        stop=(k == 3),
-                    )
-        regroup(WU + 1)
-        quantise(WU)
-        for bank in range(2):
-            dts = slice(bank * PACK, (bank + 1) * PACK)
-            nc.vector.tensor_tensor(
-                out=g_bias[:, dts, :].rearrange("p j (b s) -> p j b s", s=2),
-                in0=g_banks[bank][:].rearrange("p j (s b) -> p j b s", s=2),
-                in1=bias[:, dts].unsqueeze(2).unsqueeze(3).to_broadcast([P, PACK, WALKERS, 2]),
-                op=ADD,
+
+        def mix_g():
+            for bank in range(2):
+                g_bank = mm_ps.tile([P, PACK, P], F32, tag="mm_bank", name="g_bank")
+                g_banks.append(g_bank)
+                for j in range(PACK):
+                    dt = bank * PACK + j
+                    features = slice(dt * P, (dt + 1) * P)
+                    for k in range(4):
+                        first = 0 if k < 2 else WALKERS
+                        nc.tensor.matmul_mx(
+                            out=g_bank[:, j, :],
+                            lhsT=w_codes[:, WM + k, features].bitcast(FP8X4),
+                            lhsT_scale=w_scales[:, WM + k, features],
+                            rhs=m_codes[:, k % 2, first : first + P].bitcast(FP8X4),
+                            rhs_scale=m_scales[:, k % 2, first : first + P],
+                            start=(k == 0),
+                            stop=(k == 3),
+                        )
+
+        def add_bias():
+            for bank in range(2):
+                dts = slice(bank * PACK, (bank + 1) * PACK)
+                nc.vector.tensor_tensor(
+                    out=g_bias[:, dts, :].rearrange("p j (b s) -> p j b s", s=2),
+                    in0=g_banks[bank][:].rearrange("p j (s b) -> p j b s", s=2),
+                    in1=bias[:, dts].unsqueeze(2).unsqueeze(3).to_broadcast([P, PACK, WALKERS, 2]),
+                    op=ADD,
+                )
+
+        spreads = {}
+        g_rows = {}
+
+        def spread_g(unit):
+            spread = stage.tile([P, D_TILES, GROUPS, PACK], F32, align_bytes=64)
+            spreads[unit] = spread
+            nc.vector.tensor_copy(
+                out=spread[:],
+                in_=g_bias[:, :, unit * GROUPS : (unit + 1) * GROUPS]
+                .unsqueeze(3)
+                .to_broadcast([P, D_TILES, GROUPS, PACK]),
             )
 
-        regroup(W2)
-        quantise(WU + 1)
-        quantise(W2)
+        def turn_g(unit):
+            g_row = stage.tile([P, D1], F32, align_bytes=64)
+            g_rows[unit] = g_row
+            for half in range(2):
+                g_turned = g_ps.tile([P, PACK, P], F32, tag="g_bank")
+                for j in range(PACK):
+                    nc.tensor.transpose(
+                        g_turned[:, j, :],
+                        spreads[unit][:, half * PACK + j, :, :].rearrange("p c i -> p (c i)"),
+                        ident[:],
+                    )
+                nc.scalar.copy(
+                    out=g_row[:, half * BANK : (half + 1) * BANK],
+                    in_=g_turned[:].rearrange("p j c -> p (j c)"),
+                )
 
-        e_codes = keep.tile([P, UNITS, UNIT], U32, align_bytes=64)
-        e_scales = keep.tile([P, UNITS, UNIT], U8, align_bytes=64)
-
+        e_codes = keep.tile([P, UNITS, 2, P], U32, align_bytes=64)
+        e_scales = keep.tile([P, UNITS, 2, P], U8, align_bytes=64)
         e_grouped = {}
-        e_banks = {}
 
-        def pair_means(quarter):
-            unit = quarter // 4
-            half = quarter % 4 // 2
-            tile_index = quarter // 2
-            if quarter % 4 == 0:
-                grouped_e = stage.tile([P, UNIT, PACK], BF16, align_bytes=64)
+        def pair_means(piece):
+            unit = piece // 2
+            half = piece % 2
+            if half == 0:
+                grouped_e = stage.tile([P, 2, P, PACK], BF16, align_bytes=64)
                 e_grouped[unit] = grouped_e
-            if quarter % 2 == 0:
-                e_bank = in_ps.tile([P, PACK, P], F32, tag="in_bank")
-                e_banks[tile_index] = e_bank
-            blocks = big_tiles[SLABS + tile_index][:].rearrange("p w (j0 h c) -> p w j0 h c", j0=2, h=2)
-            by_half = e_banks[tile_index][:].rearrange("p (place h) r -> p h place r", h=2)
-            for w in range(quarter % 2 * 4, quarter % 2 * 4 + 4):
+            e_bank = in_ps.tile([P, PACK, P], F32, tag="in_bank")
+            blocks = big_tiles[SLABS + piece][:].rearrange("p w (j0 h c) -> p w j0 h c", j0=2, h=2)
+            by_half = e_bank[:].rearrange("p (place h) r -> p h place r", h=2)
+            for w in range(WALKERS_PER_TILE):
                 for h in range(2):
                     for j0 in range(2):
                         nc.tensor.matmul(
@@ -296,95 +316,158 @@ def tile_ferminetoneelectronlayer_pa_kernel(
                             start=(j0 == 0),
                             stop=(j0 == 1),
                         )
-            if quarter % 2 == 1:
-                nc.scalar.copy(
-                    out=e_grouped[unit][:, half * P : (half + 1) * P, :],
-                    in_=e_banks[tile_index][:].rearrange("p t r -> p r t"),
-                )
-            if quarter % 4 == 3:
-                nc.vector.quantize_mx(
-                    out=e_codes[:, unit, :].bitcast(FP8X4),
-                    scales=e_scales[:, unit, :],
-                    in_=e_grouped[unit][:].rearrange("p r t -> p (r t)"),
-                )
+            nc.scalar.copy(
+                out=e_grouped[unit][:, :, half * P // 2 : (half + 1) * P // 2, :],
+                in_=e_bank[:].rearrange("p t (r e) -> p e r t", e=2),
+            )
 
+        def quantise_e(unit):
+            nc.vector.quantize_mx(
+                out=e_codes[:, unit, :, :].rearrange("p e r -> p (e r)").bitcast(FP8X4),
+                scales=e_scales[:, unit, :, :].rearrange("p e r -> p (e r)"),
+                in_=e_grouped[unit][:].rearrange("p e r t -> p (e r t)"),
+            )
+
+        mm_banks = {}
         tanh_tiles = {}
 
-        def layer(step):
-            unit = step // 4
-            pair = step % 4
-            mm = mm_ps.tile([P, 2, UNIT], F32, tag="mm_bank")
-            for j in range(2):
-                dt = 2 * pair + j
-                features = slice(dt * P, (dt + 1) * P)
+        def layer_u(step):
+            unit = step // 2
+            tokens = slice(step % 2 * P, (step % 2 + 1) * P)
+            for half in range(2):
+                features = slice(half * BANK, (half + 1) * BANK)
+                mm = mm_ps.tile([P, BANK], F32, tag="mm_bank")
+                mm_banks[step, half] = mm
                 for g in range(2):
                     nc.tensor.matmul_mx(
-                        out=mm[:, j, :],
-                        lhsT=w_codes[:, WU + g, features].bitcast(FP8X4),
-                        lhsT_scale=w_scales[:, WU + g, features],
-                        rhs=x_codes[:, unit, g, :].bitcast(FP8X4),
-                        rhs_scale=x_scales[:, unit, g, :],
+                        out=mm[:],
+                        lhsT=x_codes[:, unit, g, tokens].bitcast(FP8X4),
+                        lhsT_scale=x_scales[:, unit, g, tokens],
+                        rhs=w_codes[:, WU + g, features].bitcast(FP8X4),
+                        rhs_scale=w_scales[:, WU + g, features],
                         start=(g == 0),
                         stop=False,
                     )
+
+        def layer_e(step):
+            unit = step // 2
+            for half in range(2):
+                features = slice(half * BANK, (half + 1) * BANK)
                 nc.tensor.matmul_mx(
-                    out=mm[:, j, :],
-                    lhsT=w_codes[:, W2, features].bitcast(FP8X4),
-                    lhsT_scale=w_scales[:, W2, features],
-                    rhs=e_codes[:, unit, :].bitcast(FP8X4),
-                    rhs_scale=e_scales[:, unit, :],
+                    out=mm_banks[step, half][:],
+                    lhsT=e_codes[:, unit, step % 2, :].bitcast(FP8X4),
+                    lhsT_scale=e_scales[:, unit, step % 2, :],
+                    rhs=w_codes[:, W2, features].bitcast(FP8X4),
+                    rhs_scale=w_scales[:, W2, features],
                     start=False,
                     stop=True,
                 )
-            groups = UNIT // PER_SPIN
-            total = sums.tile([P, 2, UNIT], F32)
-            nc.vector.tensor_tensor(
-                out=total[:].rearrange("p j (c i) -> p j c i", i=PER_SPIN),
-                in0=mm[:].rearrange("p j (c i) -> p j c i", i=PER_SPIN),
-                in1=g_bias[:, 2 * pair : 2 * pair + 2, unit * groups : (unit + 1) * groups]
-                .unsqueeze(3)
-                .to_broadcast([P, 2, groups, PER_SPIN]),
-                op=ADD,
-            )
-            tanh = acts.tile([P, 2, UNIT], F32)
-            nc.scalar.activation(out=tanh[:], in_=total[:], func=TANH)
-            tanh_tiles[step] = tanh
 
-        rows = {}
+        def activate(step):
+            unit = step // 2
+            total = sums.tile([P, D1], F32, tag="total", name="total")
+            for half in range(2):
+                features = slice(half * BANK, (half + 1) * BANK)
+                nc.vector.tensor_tensor(
+                    out=total[:, features],
+                    in0=mm_banks[step, half][:],
+                    in1=g_rows[unit][:, features],
+                    op=ADD,
+                )
+            tanh = acts.tile([P, D1], F32, tag="tanh", name="tanh")
+            tanh_tiles[step] = tanh
+            nc.scalar.activation(out=tanh[:], in_=total[:], func=TANH)
+
+        def end(step):
+            unit = step // 2
+            total = sums.tile([P, D1], F32, tag="total", name="total")
+            tanh = acts.tile([P, D1], F32, tag="tanh", name="tanh")
+            result = results.tile([P, D1], F32, tag="result", name="result")
+            for half in range(2):
+                features = slice(half * BANK, (half + 1) * BANK)
+                nc.vector.tensor_tensor(
+                    out=total[:, features],
+                    in0=mm_banks[step, half][:],
+                    in1=g_rows[unit][:, features],
+                    op=ADD,
+                )
+                nc.scalar.activation(out=tanh[:, features], in_=total[:, features], func=TANH)
+            for half in range(2):
+                features = slice(half * BANK, (half + 1) * BANK)
+                nc.vector.tensor_tensor(
+                    out=result[:, features],
+                    in0=tanh[:, features],
+                    in1=x1[:, unit, step % 2, features],
+                    op=ADD,
+                )
+                nc.sync.dma_start(
+                    out=out_rows[unit][:, step % 2, features], in_=result[:, features]
+                )
 
         def finish(step):
-            unit = step // 4
-            bank = step % 4 // 2
-            half = step % 2
-            tt = unit * TILES_PER_UNIT + half
-            if bank == 0:
-                result = results.tile([P, D1], F32)
-                rows[tt] = result
-            back = out_ps.tile([P, PACK, P], F32)
-            for j in range(PACK):
-                dt = bank * PACK + j
-                nc.tensor.transpose(
-                    back[:, j, :],
-                    tanh_tiles[4 * unit + dt // 2][:, dt % 2, half * P : (half + 1) * P],
-                    ident[:],
-                )
-            cols = slice(bank * BANK, (bank + 1) * BANK)
+            unit = step // 2
+            result = results.tile([P, D1], F32, tag="result", name="result")
             nc.vector.tensor_tensor(
-                out=rows[tt][:, cols],
-                in0=back[:].rearrange("p j c -> p (j c)"),
-                in1=x1[:, tt, cols],
-                op=ADD,
+                out=result[:], in0=tanh_tiles[step][:], in1=x1[:, unit, step % 2, :], op=ADD
             )
-            if bank == 1:
-                nc.sync.dma_start(out=out_rows[tt * P : (tt + 1) * P, :], in_=rows[tt][:])
+            nc.sync.dma_start(out=out_rows[unit][:, step % 2, :], in_=result[:])
 
-        steps = 4 * UNITS
-        for quarter in range(5):
-            pair_means(quarter)
-        for step in range(steps + 3):
-            if step < steps:
-                layer(step)
-            if step >= 3:
-                finish(step - 3)
-            if step + 5 < steps:
-                pair_means(step + 5)
+        regroup(0)
+        regroup(1)
+        quantise(0)
+        turn_x(0)
+        turn_x(1)
+        quantise(1)
+        quantise_x(0)
+        turn_x(2)
+        mean_m(0)
+        quantise_x(1)
+        mean_m(1)
+        turn_x(3)
+        mean_m(2)
+        mean_m(3)
+        regroup(2)
+        quantise_x(2)
+        quantise(2)
+        quantise_x(3)
+        copy_m()
+        regroup(3)
+        quantise_m()
+        quantise(3)
+        turn_bias()
+        regroup(4)
+        mix_g()
+        quantise(4)
+        regroup(5)
+        add_bias()
+        regroup(6)
+        pair_means(0)
+        spread_g(0)
+        quantise(5)
+        pair_means(1)
+        turn_g(0)
+        layer_u(0)
+        layer_u(1)
+        quantise_e(0)
+        quantise(6)
+        spread_g(1)
+        pair_means(2)
+        steps = 2 * UNITS
+        for step in range(steps - 1):
+            layer_e(step)
+            if step + 3 < steps:
+                pair_means(step + 3)
+            activate(step)
+            if step + 2 < steps:
+                layer_u(step + 2)
+            if step % 2 == 0 and step // 2 + 1 < UNITS:
+                turn_g(step // 2 + 1)
+            if step > 0:
+                finish(step - 1)
+            if step % 2 == 0 and step // 2 + 1 < UNITS:
+                quantise_e(step // 2 + 1)
+            if step % 2 == 1 and step // 2 + 2 < UNITS:
+                spread_g(step // 2 + 2)
+        layer_e(steps - 1)
+        finish(steps - 2)
+        end(steps - 1)

@@ -59,7 +59,7 @@ def tile_ferminetoneelectronlayer_pa_kernel(
         x1_rows = in_1e.rearrange("b i k -> (b i) k").rearrange("(u p e) k -> u p e k", p=P, e=2)
         out_rows = out.rearrange("b i d -> (b i) d").rearrange("(u p e) d -> u p e d", p=P, e=2)
         pair_rows = in_2e.rearrange("b i (jj j0) c -> (i jj) b (j0 c)", j0=2)
-        wm_slabs = W_mixed.rearrange("(g t p) n -> g p t n", t=PACK, p=P)
+        wm_slabs = W_mixed.rearrange("(g p t) n -> g p t n", t=PACK, p=P)
         wu_slabs = W_unmixed.rearrange("(g u q e) n -> g q u e n", u=2, q=P, e=2)
         w2_slab = W_2e.rearrange("(t p) n -> p t n", p=P)
 
@@ -204,7 +204,7 @@ def tile_ferminetoneelectronlayer_pa_kernel(
                         out=m_ps[c // PACK][:, c % PACK, :].rearrange("p (s b) -> p s b", s=2)[
                             :, :, unit * GROUPS // 2 : (unit + 1) * GROUPS // 2
                         ],
-                        lhsT=x1[:, unit, half, c * P : (c + 1) * P],
+                        lhsT=x1[:, unit, half, c // PACK * 512 + c % PACK : (c // PACK + 1) * 512 : PACK],
                         rhs=sel_m[:],
                         start=(half == 0),
                         stop=(half == 1),

@@ -24,7 +24,7 @@ UNITS = TOKENS // UNIT
 TILES_PER_UNIT = UNIT // P
 D_TILES = D1 // P
 BANK = 512
-V_COLS = (640, 640, 640, 384, 384, 384, 384)
+V_COLS = (512, 512, 512, 512, 512, 512, 512)
 WALKERS_PER_TILE = P // ELECTRONS
 GROUPS = UNIT // PER_SPIN
 
@@ -50,7 +50,7 @@ def tile_ferminetoneelectronlayer_pa_kernel(
         stage = ctx.enter_context(tc.tile_pool(name="stage", bufs=2))
         sums = ctx.enter_context(tc.tile_pool(name="sums", bufs=2))
         acts = ctx.enter_context(tc.tile_pool(name="acts", bufs=2))
-        results = ctx.enter_context(tc.tile_pool(name="results", bufs=3))
+        results = ctx.enter_context(tc.tile_pool(name="results", bufs=4))
         in_ps = ctx.enter_context(tc.psum_pool(name="in_ps", bufs=2))
         mm_ps = ctx.enter_context(tc.psum_pool(name="mm_ps", bufs=4))
         g_ps = ctx.enter_context(tc.psum_pool(name="g_ps", bufs=2))
@@ -73,10 +73,7 @@ def tile_ferminetoneelectronlayer_pa_kernel(
         def load_big(j):
             if j < SLABS:
                 raw = big.tile([P, PACK, D1], BF16, tag="big", name="raw")
-                if j == 0:
-                    for cols in (slice(0, V_COLS[0]), slice(V_COLS[0], D1)):
-                        nc.sync.dma_start(out=raw[:, :, cols], in_=wm_slabs[0][:, :, cols])
-                elif j < WU:
+                if j < WU:
                     nc.sync.dma_start(out=raw[:], in_=wm_slabs[j - WM])
                 elif j < W2:
                     for u in range(2):
@@ -91,11 +88,11 @@ def tile_ferminetoneelectronlayer_pa_kernel(
                 nc.sync.dma_start(out=raw[:], in_=pair_rows[:, first : first + WALKERS_PER_TILE, :])
             big_tiles[j] = raw
 
-        load_big(0)
-        load_big(1)
+        for j in range(3):
+            load_big(j)
         for unit in range(UNITS):
             nc.sync.dma_start(out=x1[:, unit, :, :], in_=x1_rows[unit])
-        for j in range(2, BIG_BUFS):
+        for j in range(3, BIG_BUFS):
             load_big(j)
 
         dummy = const.tile([P, 1], F32)
@@ -155,11 +152,12 @@ def tile_ferminetoneelectronlayer_pa_kernel(
             if k + BIG_BUFS < BIG_LOADS:
                 load_big(k + BIG_BUFS)
 
-        def quantise(k):
+        def quantise(k, half):
+            cols = slice(half * BANK, (half + 1) * BANK)
             nc.vector.quantize_mx(
-                out=w_codes[:, k, :].bitcast(FP8X4),
-                scales=w_scales[:, k, :],
-                in_=w_grouped[k][:].rearrange("p n t -> p (n t)"),
+                out=w_codes[:, k, cols].bitcast(FP8X4),
+                scales=w_scales[:, k, cols],
+                in_=w_grouped[k][:, cols, :].rearrange("p n t -> p (n t)"),
             )
 
         x_codes = keep.tile([P, UNITS, 2, UNIT], U32, align_bytes=64)
@@ -378,11 +376,11 @@ def tile_ferminetoneelectronlayer_pa_kernel(
             tanh_tiles[step] = tanh
             nc.scalar.activation(out=tanh[:], in_=total[:], func=TANH)
 
-        def end(step):
+        def activate_halves(step):
             unit = step // 2
             total = sums.tile([P, D1], F32, tag="total", name="total")
             tanh = acts.tile([P, D1], F32, tag="tanh", name="tanh")
-            result = results.tile([P, D1], F32, tag="result", name="result")
+            tanh_tiles[step] = tanh
             for half in range(2):
                 features = slice(half * BANK, (half + 1) * BANK)
                 nc.vector.tensor_tensor(
@@ -392,11 +390,15 @@ def tile_ferminetoneelectronlayer_pa_kernel(
                     op=ADD,
                 )
                 nc.scalar.activation(out=tanh[:, features], in_=total[:, features], func=TANH)
+
+        def finish_halves(step):
+            unit = step // 2
+            result = results.tile([P, D1], F32, tag="result", name="result")
             for half in range(2):
                 features = slice(half * BANK, (half + 1) * BANK)
                 nc.vector.tensor_tensor(
                     out=result[:, features],
-                    in0=tanh[:, features],
+                    in0=tanh_tiles[step][:, features],
                     in1=x1[:, unit, step % 2, features],
                     op=ADD,
                 )
@@ -413,61 +415,72 @@ def tile_ferminetoneelectronlayer_pa_kernel(
             nc.sync.dma_start(out=out_rows[unit][:, step % 2, :], in_=result[:])
 
         regroup(0)
+        quantise(0, 0)
         regroup(1)
-        quantise(0)
+        quantise(0, 1)
+        quantise(1, 0)
+        regroup(2)
+        quantise(1, 1)
         turn_x(0)
         turn_x(1)
-        quantise(1)
+        quantise(2, 0)
         quantise_x(0)
+        quantise(2, 1)
         turn_x(2)
+        turn_x(3)
         mean_m(0)
         quantise_x(1)
         mean_m(1)
-        turn_x(3)
         mean_m(2)
         mean_m(3)
-        regroup(2)
-        quantise_x(2)
-        quantise(2)
-        quantise_x(3)
-        copy_m()
         regroup(3)
-        quantise_m()
-        quantise(3)
-        turn_bias()
+        quantise_x(2)
+        quantise(3, 0)
+        quantise_x(3)
+        quantise(3, 1)
+        copy_m()
         regroup(4)
+        quantise_m()
+        turn_bias()
+        quantise(4, 0)
         mix_g()
-        quantise(4)
         regroup(5)
-        add_bias()
-        regroup(6)
+        quantise(4, 1)
+        quantise(5, 0)
         pair_means(0)
+        regroup(6)
+        quantise(5, 1)
+        layer_u(0)
+        add_bias()
         spread_g(0)
-        quantise(5)
         pair_means(1)
         turn_g(0)
-        layer_u(0)
-        layer_u(1)
+        quantise(6, 0)
+        quantise(6, 1)
         quantise_e(0)
-        quantise(6)
-        spread_g(1)
-        pair_means(2)
         steps = 2 * UNITS
         for step in range(steps - 1):
             layer_e(step)
+            if step == 0:
+                layer_u(1)
+                pair_means(2)
+            if step + 2 < steps:
+                layer_u(step + 2)
             if step + 3 < steps:
                 pair_means(step + 3)
             activate(step)
-            if step + 2 < steps:
-                layer_u(step + 2)
+            if step == 0:
+                spread_g(1)
             if step % 2 == 0 and step // 2 + 1 < UNITS:
                 turn_g(step // 2 + 1)
-            if step > 0:
+            if 0 < step < steps - 2:
                 finish(step - 1)
             if step % 2 == 0 and step // 2 + 1 < UNITS:
                 quantise_e(step // 2 + 1)
             if step % 2 == 1 and step // 2 + 2 < UNITS:
                 spread_g(step // 2 + 2)
         layer_e(steps - 1)
+        finish(steps - 3)
+        activate_halves(steps - 1)
         finish(steps - 2)
-        end(steps - 1)
+        finish_halves(steps - 1)

@@ -409,7 +409,8 @@ def tile_ferminetoneelectronlayer_pa_kernel(
         def finish(step):
             unit = step // 2
             result = results.tile([P, D1], F32, tag="result", name="result")
-            nc.vector.tensor_tensor(
+            engine = nc.gpsimd if step == 2 * UNITS - 3 else nc.vector
+            engine.tensor_tensor(
                 out=result[:], in0=tanh_tiles[step][:], in1=x1[:, unit, step % 2, :], op=ADD
             )
             nc.sync.dma_start(out=out_rows[unit][:, step % 2, :], in_=result[:])
@@ -464,13 +465,13 @@ def tile_ferminetoneelectronlayer_pa_kernel(
             if step == 0:
                 layer_u(1)
                 pair_means(2)
-            if step + 2 < steps:
-                layer_u(step + 2)
             if step + 3 < steps:
                 pair_means(step + 3)
             activate(step)
             if step == 0:
                 spread_g(1)
+            if step + 2 < steps:
+                layer_u(step + 2)
             if step % 2 == 0 and step // 2 + 1 < UNITS:
                 turn_g(step // 2 + 1)
             if 0 < step < steps - 2:

@@ -448,40 +448,39 @@ def tile_ferminetoneelectronlayer_pa_kernel(
         regroup(5)
         quantise(4, 1)
         quantise(5, 0)
-        pair_means(0)
         regroup(6)
         quantise(5, 1)
+        pair_means(0)
         layer_u(0)
+        pair_means(1)
         add_bias()
         spread_g(0)
-        pair_means(1)
         turn_g(0)
         quantise(6, 0)
         quantise(6, 1)
         quantise_e(0)
+        spread_g(1)
         steps = 2 * UNITS
         for step in range(steps - 1):
+            unit = step // 2
             layer_e(step)
-            if step == 0:
-                layer_u(1)
-                pair_means(2)
-            if step + 3 < steps:
-                pair_means(step + 3)
-            activate(step)
-            if step == 0:
-                spread_g(1)
             if step + 2 < steps:
-                layer_u(step + 2)
-            if step % 2 == 0 and step // 2 + 1 < UNITS:
-                turn_g(step // 2 + 1)
-            if 0 < step < steps - 2:
-                finish(step - 1)
-            if step % 2 == 0 and step // 2 + 1 < UNITS:
-                quantise_e(step // 2 + 1)
-            if step % 2 == 1 and step // 2 + 2 < UNITS:
-                spread_g(step // 2 + 2)
+                pair_means(step + 2)
+            layer_u(step + 1)
+            if step > 1:
+                finish(step - 2)
+            if step < steps - 2:
+                activate(step)
+            else:
+                activate_halves(step)
+            if step % 2 == 1 and unit + 1 < UNITS:
+                turn_g(unit + 1)
+            if step % 2 == 1:
+                quantise_e(unit + 1)
+            if step % 2 == 0 and unit + 2 < UNITS:
+                spread_g(unit + 2)
         layer_e(steps - 1)
         finish(steps - 3)
         activate_halves(steps - 1)
-        finish(steps - 2)
+        finish_halves(steps - 2)
         finish_halves(steps - 1)

@@ -24,7 +24,7 @@ UNITS = TOKENS // UNIT
 TILES_PER_UNIT = UNIT // P
 D_TILES = D1 // P
 BANK = 512
-V_COLS = (512, 512, 512, 512, 512, 512, 512)
+V_COLS = (576, 512, 512, 512, 512, 448, 384)
 WALKERS_PER_TILE = P // ELECTRONS
 GROUPS = UNIT // PER_SPIN
 
@@ -85,7 +85,13 @@ def tile_ferminetoneelectronlayer_pa_kernel(
             else:
                 first = (j - SLABS) * WALKERS_PER_TILE
                 raw = big.tile([P, WALKERS_PER_TILE, 2 * D2], BF16, tag="big", name="raw")
-                nc.sync.dma_start(out=raw[:], in_=pair_rows[:, first : first + WALKERS_PER_TILE, :])
+                parts = 2 if j >= SLABS and (j - SLABS) % 2 == 1 else 1
+                walkers = WALKERS_PER_TILE // parts
+                for part in range(parts):
+                    nc.sync.dma_start(
+                        out=raw[:, part * walkers : (part + 1) * walkers, :],
+                        in_=pair_rows[:, first + part * walkers : first + (part + 1) * walkers, :],
+                    )
             big_tiles[j] = raw
 
         for j in range(3):
@@ -409,7 +415,7 @@ def tile_ferminetoneelectronlayer_pa_kernel(
         def finish(step):
             unit = step // 2
             result = results.tile([P, D1], F32, tag="result", name="result")
-            engine = nc.gpsimd if step == 2 * UNITS - 3 else nc.vector
+            engine = nc.gpsimd if step in (3, 5) else nc.vector
             engine.tensor_tensor(
                 out=result[:], in0=tanh_tiles[step][:], in1=x1[:, unit, step % 2, :], op=ADD
             )

@@ -60,8 +60,8 @@ def tile_ferminetoneelectronlayer_pa_kernel(
         out_rows = out.rearrange("b i d -> (b i) d").rearrange("(u p e) d -> u p e d", p=P, e=2)
         pair_rows = in_2e.rearrange("b i (jj j0) c -> (i jj) b (j0 c)", j0=2)
         wm_slabs = W_mixed.rearrange("(g p t) n -> g p t n", t=PACK, p=P)
-        wu_slabs = W_unmixed.rearrange("(g u q e) n -> g q u e n", u=2, q=P, e=2)
-        w2_slab = W_2e.rearrange("(t p) n -> p t n", p=P)
+        wu_slabs = W_unmixed.rearrange("(g p t) n -> g p t n", t=PACK, p=P)
+        w2_slab = W_2e.rearrange("(place p e) n -> p place e n", p=P, e=2)
 
         bias_rows = const.tile([P, P], BF16)
         nc.vector.memset(bias_rows[:], 0.0)
@@ -76,12 +76,11 @@ def tile_ferminetoneelectronlayer_pa_kernel(
                 if j < WU:
                     nc.sync.dma_start(out=raw[:], in_=wm_slabs[j - WM])
                 elif j < W2:
-                    for u in range(2):
-                        nc.sync.dma_start(
-                            out=raw[:, 2 * u : 2 * u + 2, :], in_=wu_slabs[j - WU][:, u, :, :]
-                        )
+                    nc.sync.dma_start(out=raw[:], in_=wu_slabs[j - WU])
                 else:
-                    nc.sync.dma_start(out=raw[:], in_=w2_slab)
+                    nc.sync.dma_start(
+                        out=raw[:].rearrange("p (place e) n -> p place e n", e=2), in_=w2_slab
+                    )
             else:
                 first = (j - SLABS) * WALKERS_PER_TILE
                 raw = big.tile([P, WALKERS_PER_TILE, 2 * D2], BF16, tag="big", name="raw")
@@ -179,7 +178,10 @@ def tile_ferminetoneelectronlayer_pa_kernel(
                 ps, tag = ((in_ps, "in_bank"), (g_ps, "g_bank"))[half]
                 xt = ps.tile([P, PACK, P], F32, tag=tag, name="xt")
                 for c in range(PACK):
-                    nc.tensor.transpose(xt[:, c, :], words[:, c * P : (c + 1) * P], ident[:])
+                    first = c // 2 * 2 * P + c % 2
+                    nc.tensor.transpose(
+                        xt[:, c, :], words[:, first : (c // 2 + 1) * 2 * P : 2], ident[:]
+                    )
                 nc.scalar.copy(
                     out=grouped_x[:].bitcast(F32)[:, :, tokens, :],
                     in_=xt[:].rearrange("p (g u) r -> p g r u", u=2),
@@ -308,17 +310,17 @@ def tile_ferminetoneelectronlayer_pa_kernel(
                 grouped_e = stage.tile([P, 2, P, PACK], BF16, align_bytes=64)
                 e_grouped[unit] = grouped_e
             e_bank = in_ps.tile([P, PACK, P], F32, tag="in_bank")
-            blocks = big_tiles[SLABS + piece][:].rearrange("p w (j0 h c) -> p w j0 h c", j0=2, h=2)
-            by_half = e_bank[:].rearrange("p (place h) r -> p h place r", h=2)
+            blocks = big_tiles[SLABS + piece][:].rearrange("p w (j c e) -> p w j e c", j=2, e=2)
+            by_parity = e_bank[:].rearrange("p (place e) r -> p e place r", e=2)
             for w in range(WALKERS_PER_TILE):
-                for h in range(2):
-                    for j0 in range(2):
+                for e in range(2):
+                    for j in range(2):
                         nc.tensor.matmul(
-                            out=by_half[:, h, :, w * ELECTRONS : (w + 1) * ELECTRONS],
-                            lhsT=blocks[:, w, j0, h, :],
+                            out=by_parity[:, e, :, w * ELECTRONS : (w + 1) * ELECTRONS],
+                            lhsT=blocks[:, w, j, e, :],
                             rhs=sel_2[:],
-                            start=(j0 == 0),
-                            stop=(j0 == 1),
+                            start=(j == 0),
+                            stop=(j == 1),
                         )
             nc.scalar.copy(
                 out=e_grouped[unit][:, :, half * P // 2 : (half + 1) * P // 2, :],

from contextlib import ExitStack

import concourse.mybir as mybir
from concourse.masks import make_identity

F32 = mybir.dt.float32
BF16 = mybir.dt.bfloat16
U32 = mybir.dt.uint32
U8 = mybir.dt.uint8
FP8X4 = mybir.dt.float8_e4m3fn_x4
ADD = mybir.AluOpType.add
TANH = mybir.ActivationFunctionType.Tanh

P = 128
PACK = 4
WALKERS = 64
ELECTRONS = 16
PER_SPIN = 8
D1 = 1024
D2 = 256
TOKENS = WALKERS * ELECTRONS
UNIT = 256
UNITS = TOKENS // UNIT
TILES_PER_UNIT = UNIT // P
D_TILES = D1 // P
BANK = 512
V_COLS = (576, 512, 512, 512, 512, 448, 384)
WALKERS_PER_TILE = P // ELECTRONS
GROUPS = UNIT // PER_SPIN

WM = 0
WU = 4
W2 = 6
SLABS = 7
PAIR_TILES = TOKENS // P
BIG_LOADS = SLABS + PAIR_TILES
BIG_BUFS = 9

FLOPS = 2 * (TOKENS * D1 * D1 + 2 * WALKERS * 2 * D1 * D1 + TOKENS * 2 * D2 * D1)


def tile_ferminetoneelectronlayer_pa_kernel(
    tc, in_1e, in_2e, W_unmixed, b_unmixed, W_mixed, W_2e, out
):
    nc = tc.nc
    with ExitStack() as ctx:
        const = ctx.enter_context(tc.tile_pool(name="const", bufs=1))
        keep = ctx.enter_context(tc.tile_pool(name="keep", bufs=1))
        big = ctx.enter_context(tc.tile_pool(name="big", bufs=BIG_BUFS))
        stage = ctx.enter_context(tc.tile_pool(name="stage", bufs=2))
        sums = ctx.enter_context(tc.tile_pool(name="sums", bufs=2))
        acts = ctx.enter_context(tc.tile_pool(name="acts", bufs=2))
        results = ctx.enter_context(tc.tile_pool(name="results", bufs=4))
        in_ps = ctx.enter_context(tc.psum_pool(name="in_ps", bufs=2))
        mm_ps = ctx.enter_context(tc.psum_pool(name="mm_ps", bufs=4))
        g_ps = ctx.enter_context(tc.psum_pool(name="g_ps", bufs=2))
        ctx.enter_context(tc.manual_schedule())

        x1_rows = in_1e.rearrange("b i k -> (b i) k").rearrange("(u p e) k -> u p e k", p=P, e=2)
        out_rows = out.rearrange("b i d -> (b i) d").rearrange("(u p e) d -> u p e d", p=P, e=2)
        pair_rows = in_2e.rearrange("b i (jj j0) c -> (i jj) b (j0 c)", j0=2)
        wm_slabs = W_mixed.rearrange("(g p t) n -> g p t n", t=PACK, p=P)
        wu_slabs = W_unmixed.rearrange("(g p t) n -> g p t n", t=PACK, p=P)
        w2_slab = W_2e.rearrange("(place p e) n -> p place e n", p=P, e=2)

        bias_rows = const.tile([P, P], BF16)
        nc.vector.memset(bias_rows[:], 0.0)
        nc.scalar.dma_start(out=bias_rows[0:D_TILES, :], in_=b_unmixed.rearrange("(r c) -> r c", c=P))
        x1 = keep.tile([P, UNITS, 2, D1], BF16)

        big_tiles = {}

        def load_big(j):
            if j < SLABS:
                raw = big.tile([P, PACK, D1], BF16, tag="big", name="raw")
                if j < WU:
                    nc.sync.dma_start(out=raw[:], in_=wm_slabs[j - WM])
                elif j < W2:
                    nc.sync.dma_start(out=raw[:], in_=wu_slabs[j - WU])
                else:
                    nc.sync.dma_start(
                        out=raw[:].rearrange("p (place e) n -> p place e n", e=2), in_=w2_slab
                    )
            else:
                first = (j - SLABS) * WALKERS_PER_TILE
                raw = big.tile([P, WALKERS_PER_TILE, 2 * D2], BF16, tag="big", name="raw")
                parts = 2 if j >= SLABS and (j - SLABS) % 2 == 1 else 1
                walkers = WALKERS_PER_TILE // parts
                for part in range(parts):
                    nc.sync.dma_start(
                        out=raw[:, part * walkers : (part + 1) * walkers, :],
                        in_=pair_rows[:, first + part * walkers : first + (part + 1) * walkers, :],
                    )
            big_tiles[j] = raw

        for j in range(3):
            load_big(j)
        for unit in range(UNITS):
            nc.sync.dma_start(out=x1[:, unit, :, :], in_=x1_rows[unit])
        for j in range(3, BIG_BUFS):
            load_big(j)

        dummy = const.tile([P, 1], F32)
        nc.vector.memset(dummy[:], 0.0)
        nc.scalar.activation(out=dummy[:], in_=dummy[:], func=TANH)
        ident = const.tile([P, P], F32)
        make_identity(nc, ident[:])
        ident_bf = const.tile([P, P], BF16)
        nc.vector.tensor_copy(out=ident_bf[:], in_=ident[:])

        hit_m = const.tile([P, GROUPS], F32)
        nc.vector.tensor_reduce(
            out=hit_m[:],
            in_=ident[:].rearrange("p (q i) -> p q i", i=PER_SPIN // 2),
            axis=mybir.AxisListType.X,
            op=ADD,
        )
        sel_m = const.tile([P, 2, GROUPS // 2], BF16)
        nc.vector.tensor_scalar_mul(
            out=sel_m[:], in0=hit_m[:].rearrange("p (b s) -> p s b", s=2), scalar1=1.0 / PER_SPIN
        )

        hit_2 = const.tile([P, 2 * ELECTRONS], F32)
        nc.vector.tensor_reduce(
            out=hit_2[:],
            in_=ident[:].rearrange("p (q j) -> p q j", j=PER_SPIN // 2),
            axis=mybir.AxisListType.X,
            op=ADD,
        )
        hit_2_by_spin = hit_2[:].rearrange("p (r i c) -> p r c i", r=2, c=2)
        sel_2 = const.tile([P, 2, ELECTRONS], BF16)
        for row_spin in range(2):
            for place in range(2):
                nc.vector.tensor_scalar_mul(
                    out=sel_2[:, place, row_spin * PER_SPIN : (row_spin + 1) * PER_SPIN],
                    in0=hit_2_by_spin[:, row_spin, (row_spin + place) % 2, :],
                    scalar1=1.0 / PER_SPIN,
                )

        w_codes = keep.tile([P, SLABS, D1], U32, align_bytes=64)
        w_scales = keep.tile([P, SLABS, D1], U8, align_bytes=64)
        w_grouped = {}

        def regroup(k):
            raw = big_tiles[k]
            grouped = stage.tile([P, D1, PACK], BF16, align_bytes=64, bufs=3)
            w_grouped[k] = grouped
            mid = V_COLS[k]
            nc.vector.tensor_copy(
                out=grouped[:, 0:mid, :].rearrange("p (c i) t -> p c t i", i=4),
                in_=raw[:, :, 0:mid].rearrange("p t (c i) -> p c t i", i=4),
            )
            nc.scalar.copy(
                out=grouped[:, mid:D1, :].rearrange("p (c i) t -> p c t i", i=4),
                in_=raw[:, :, mid:D1].rearrange("p t (c i) -> p c t i", i=4),
            )
            if k + BIG_BUFS < BIG_LOADS:
                load_big(k + BIG_BUFS)

        def quantise(k, half):
            cols = slice(half * BANK, (half + 1) * BANK)
            nc.vector.quantize_mx(
                out=w_codes[:, k, cols].bitcast(FP8X4),
                scales=w_scales[:, k, cols],
                in_=w_grouped[k][:, cols, :].rearrange("p n t -> p (n t)"),
            )

        x_codes = keep.tile([P, UNITS, 2, UNIT], U32, align_bytes=64)
        x_scales = keep.tile([P, UNITS, 2, UNIT], U8, align_bytes=64)
        x_grouped = {}

        def turn_x(unit):
            grouped_x = stage.tile([P, 2, UNIT, PACK], BF16, align_bytes=64)
            x_grouped[unit] = grouped_x
            for half in range(TILES_PER_UNIT):
                tokens = slice(half * P, (half + 1) * P)
                words = x1[:, unit, half, :].bitcast(F32)
                ps, tag = ((in_ps, "in_bank"), (g_ps, "g_bank"))[half]
                xt = ps.tile([P, PACK, P], F32, tag=tag, name="xt")
                for c in range(PACK):
                    first = c // 2 * 2 * P + c % 2
                    nc.tensor.transpose(
                        xt[:, c, :], words[:, first : (c // 2 + 1) * 2 * P : 2], ident[:]
                    )
                nc.scalar.copy(
                    out=grouped_x[:].bitcast(F32)[:, :, tokens, :],
                    in_=xt[:].rearrange("p (g u) r -> p g r u", u=2),
                )

        def quantise_x(unit):
            nc.vector.quantize_mx(
                out=x_codes[:, unit, :, :].rearrange("p g r -> p (g r)").bitcast(FP8X4),
                scales=x_scales[:, unit, :, :].rearrange("p g r -> p (g r)"),
                in_=x_grouped[unit][:].rearrange("p g r t -> p (g r t)"),
            )

        m_ps = []
        m_grouped = keep.tile([P, 2, 2 * P, PACK], BF16, align_bytes=64)
        m_codes = keep.tile([P, 2, 2 * P], U32, align_bytes=64)
        m_scales = keep.tile([P, 2, 2 * P], U8, align_bytes=64)

        def mean_m(unit):
            if unit == 0:
                for g in range(2):
                    m_bank = mm_ps.tile([P, PACK, P], F32, tag="mm_bank", name="m_bank")
                    m_ps.append(m_bank)
            for c in range(D1 // P):
                for half in range(2):
                    nc.tensor.matmul(
                        out=m_ps[c // PACK][:, c % PACK, :].rearrange("p (s b) -> p s b", s=2)[
                            :, :, unit * GROUPS // 2 : (unit + 1) * GROUPS // 2
                        ],
                        lhsT=x1[:, unit, half, c // PACK * 512 + c % PACK : (c // PACK + 1) * 512 : PACK],
                        rhs=sel_m[:],
                        start=(half == 0),
                        stop=(half == 1),
                    )

        def copy_m():
            for g in range(2):
                nc.scalar.copy(
                    out=m_grouped[:, g, 0:P, :],
                    in_=m_ps[g][:].rearrange("p t c -> p c t"),
                )

        def quantise_m():
            nc.vector.tensor_copy(out=m_grouped[:, :, P : 2 * P, :], in_=m_grouped[:, :, 0:P, :])
            nc.vector.quantize_mx(
                out=m_codes[:].rearrange("p g c -> p (g c)").bitcast(FP8X4),
                scales=m_scales[:].rearrange("p g c -> p (g c)"),
                in_=m_grouped[:].rearrange("p g c t -> p (g c t)"),
            )

        bias = const.tile([P, D_TILES], F32)

        def turn_bias():
            bias_ps = in_ps.tile([P, P], BF16, tag="in_bank")
            nc.tensor.transpose(bias_ps[:], bias_rows[:], ident_bf[:])
            nc.vector.tensor_copy(out=bias[:], in_=bias_ps[:, 0:D_TILES])

        g_bias = keep.tile([P, D_TILES, P], F32)
        g_banks = []

        def mix_g():
            for bank in range(2):
                g_bank = mm_ps.tile([P, PACK, P], F32, tag="mm_bank", name="g_bank")
                g_banks.append(g_bank)
                for j in range(PACK):
                    dt = bank * PACK + j
                    features = slice(dt * P, (dt + 1) * P)
                    for k in range(4):
                        first = 0 if k < 2 else WALKERS
                        nc.tensor.matmul_mx(
                            out=g_bank[:, j, :],
                            lhsT=w_codes[:, WM + k, features].bitcast(FP8X4),
                            lhsT_scale=w_scales[:, WM + k, features],
                            rhs=m_codes[:, k % 2, first : first + P].bitcast(FP8X4),
                            rhs_scale=m_scales[:, k % 2, first : first + P],
                            start=(k == 0),
                            stop=(k == 3),
                        )

        def add_bias():
            for bank in range(2):
                dts = slice(bank * PACK, (bank + 1) * PACK)
                nc.vector.tensor_tensor(
                    out=g_bias[:, dts, :].rearrange("p j (b s) -> p j b s", s=2),
                    in0=g_banks[bank][:].rearrange("p j (s b) -> p j b s", s=2),
                    in1=bias[:, dts].unsqueeze(2).unsqueeze(3).to_broadcast([P, PACK, WALKERS, 2]),
                    op=ADD,
                )

        spreads = {}
        g_rows = {}

        def spread_g(unit):
            spread = stage.tile([P, D_TILES, GROUPS, PACK], F32, align_bytes=64)
            spreads[unit] = spread
            nc.vector.tensor_copy(
                out=spread[:],
                in_=g_bias[:, :, unit * GROUPS : (unit + 1) * GROUPS]
                .unsqueeze(3)
                .to_broadcast([P, D_TILES, GROUPS, PACK]),
            )

        def turn_g(unit):
            g_row = stage.tile([P, D1], F32, align_bytes=64)
            g_rows[unit] = g_row
            for half in range(2):
                g_turned = g_ps.tile([P, PACK, P], F32, tag="g_bank")
                for j in range(PACK):
                    nc.tensor.transpose(
                        g_turned[:, j, :],
                        spreads[unit][:, half * PACK + j, :, :].rearrange("p c i -> p (c i)"),
                        ident[:],
                    )
                nc.scalar.copy(
                    out=g_row[:, half * BANK : (half + 1) * BANK],
                    in_=g_turned[:].rearrange("p j c -> p (j c)"),
                )

        e_codes = keep.tile([P, UNITS, 2, P], U32, align_bytes=64)
        e_scales = keep.tile([P, UNITS, 2, P], U8, align_bytes=64)
        e_grouped = {}

        def pair_means(piece):
            unit = piece // 2
            half = piece % 2
            if half == 0:
                grouped_e = stage.tile([P, 2, P, PACK], BF16, align_bytes=64)
                e_grouped[unit] = grouped_e
            e_bank = in_ps.tile([P, PACK, P], F32, tag="in_bank")
            blocks = big_tiles[SLABS + piece][:].rearrange("p w (j c e) -> p w j e c", j=2, e=2)
            by_parity = e_bank[:].rearrange("p (place e) r -> p e place r", e=2)
            for w in range(WALKERS_PER_TILE):
                for e in range(2):
                    for j in range(2):
                        nc.tensor.matmul(
                            out=by_parity[:, e, :, w * ELECTRONS : (w + 1) * ELECTRONS],
                            lhsT=blocks[:, w, j, e, :],
                            rhs=sel_2[:],
                            start=(j == 0),
                            stop=(j == 1),
                        )
            nc.scalar.copy(
                out=e_grouped[unit][:, :, half * P // 2 : (half + 1) * P // 2, :],
                in_=e_bank[:].rearrange("p t (r e) -> p e r t", e=2),
            )

        def quantise_e(unit):
            nc.vector.quantize_mx(
                out=e_codes[:, unit, :, :].rearrange("p e r -> p (e r)").bitcast(FP8X4),
                scales=e_scales[:, unit, :, :].rearrange("p e r -> p (e r)"),
                in_=e_grouped[unit][:].rearrange("p e r t -> p (e r t)"),
            )

        mm_banks = {}
        tanh_tiles = {}

        def layer_u(step):
            unit = step // 2
            tokens = slice(step % 2 * P, (step % 2 + 1) * P)
            for half in range(2):
                features = slice(half * BANK, (half + 1) * BANK)
                mm = mm_ps.tile([P, BANK], F32, tag="mm_bank")
                mm_banks[step, half] = mm
                for g in range(2):
                    nc.tensor.matmul_mx(
                        out=mm[:],
                        lhsT=x_codes[:, unit, g, tokens].bitcast(FP8X4),
                        lhsT_scale=x_scales[:, unit, g, tokens],
                        rhs=w_codes[:, WU + g, features].bitcast(FP8X4),
                        rhs_scale=w_scales[:, WU + g, features],
                        start=(g == 0),
                        stop=False,
                    )

        def layer_e(step):
            unit = step // 2
            for half in range(2):
                features = slice(half * BANK, (half + 1) * BANK)
                nc.tensor.matmul_mx(
                    out=mm_banks[step, half][:],
                    lhsT=e_codes[:, unit, step % 2, :].bitcast(FP8X4),
                    lhsT_scale=e_scales[:, unit, step % 2, :],
                    rhs=w_codes[:, W2, features].bitcast(FP8X4),
                    rhs_scale=w_scales[:, W2, features],
                    start=False,
                    stop=True,
                )

        def activate(step):
            unit = step // 2
            total = sums.tile([P, D1], F32, tag="total", name="total")
            for half in range(2):
                features = slice(half * BANK, (half + 1) * BANK)
                nc.vector.tensor_tensor(
                    out=total[:, features],
                    in0=mm_banks[step, half][:],
                    in1=g_rows[unit][:, features],
                    op=ADD,
                )
            tanh = acts.tile([P, D1], F32, tag="tanh", name="tanh")
            tanh_tiles[step] = tanh
            nc.scalar.activation(out=tanh[:], in_=total[:], func=TANH)

        def activate_halves(step):
            unit = step // 2
            total = sums.tile([P, D1], F32, tag="total", name="total")
            tanh = acts.tile([P, D1], F32, tag="tanh", name="tanh")
            tanh_tiles[step] = tanh
            for half in range(2):
                features = slice(half * BANK, (half + 1) * BANK)
                nc.vector.tensor_tensor(
                    out=total[:, features],
                    in0=mm_banks[step, half][:],
                    in1=g_rows[unit][:, features],
                    op=ADD,
                )
                nc.scalar.activation(out=tanh[:, features], in_=total[:, features], func=TANH)

        def finish_halves(step):
            unit = step // 2
            result = results.tile([P, D1], F32, tag="result", name="result")
            for half in range(2):
                features = slice(half * BANK, (half + 1) * BANK)
                nc.vector.tensor_tensor(
                    out=result[:, features],
                    in0=tanh_tiles[step][:, features],
                    in1=x1[:, unit, step % 2, features],
                    op=ADD,
                )
                nc.sync.dma_start(
                    out=out_rows[unit][:, step % 2, features], in_=result[:, features]
                )

        def finish(step):
            unit = step // 2
            result = results.tile([P, D1], F32, tag="result", name="result")
            engine = nc.gpsimd if step in (3, 5) else nc.vector
            engine.tensor_tensor(
                out=result[:], in0=tanh_tiles[step][:], in1=x1[:, unit, step % 2, :], op=ADD
            )
            nc.sync.dma_start(out=out_rows[unit][:, step % 2, :], in_=result[:])

        regroup(0)
        quantise(0, 0)
        regroup(1)
        quantise(0, 1)
        quantise(1, 0)
        regroup(2)
        quantise(1, 1)
        turn_x(0)
        turn_x(1)
        quantise(2, 0)
        quantise_x(0)
        quantise(2, 1)
        turn_x(2)
        turn_x(3)
        mean_m(0)
        quantise_x(1)
        mean_m(1)
        mean_m(2)
        mean_m(3)
        regroup(3)
        quantise_x(2)
        quantise(3, 0)
        quantise_x(3)
        quantise(3, 1)
        copy_m()
        regroup(4)
        quantise_m()
        turn_bias()
        quantise(4, 0)
        mix_g()
        regroup(5)
        quantise(4, 1)
        quantise(5, 0)
        regroup(6)
        quantise(5, 1)
        pair_means(0)
        layer_u(0)
        pair_means(1)
        add_bias()
        spread_g(0)
        turn_g(0)
        quantise(6, 0)
        quantise(6, 1)
        quantise_e(0)
        spread_g(1)
        steps = 2 * UNITS
        for step in range(steps - 1):
            unit = step // 2
            layer_e(step)
            if step + 2 < steps:
                pair_means(step + 2)
            layer_u(step + 1)
            if step > 1:
                finish(step - 2)
            if step < steps - 2:
                activate(step)
            else:
                activate_halves(step)
            if step % 2 == 1 and unit + 1 < UNITS:
                turn_g(unit + 1)
            if step % 2 == 1:
                quantise_e(unit + 1)
            if step % 2 == 0 and unit + 2 < UNITS:
                spread_g(unit + 2)
        layer_e(steps - 1)
        finish(steps - 3)
        activate_halves(steps - 1)
        finish_halves(steps - 2)
        finish_halves(steps - 1)
